import numpy as np
import ml_dtypes


def mxq(x, axis, fmt="e4m3"):
    dtype, down = {"e4m3": (ml_dtypes.float8_e4m3fn, 7), "e5m2": (ml_dtypes.float8_e5m2, 14)}[fmt]
    v = np.moveaxis(np.asarray(x, np.float32).astype(ml_dtypes.bfloat16).astype(np.float64), axis, -1)
    blocks = v.reshape(v.shape[:-1] + (-1, 32))
    amax = np.abs(blocks).max(-1, keepdims=True)
    byte = np.maximum(np.where(amax > 0, np.frexp(amax)[1] - 1 + 127, 0) - down, 1)
    scale = np.exp2(byte - 127.0)
    codes = (blocks / scale).astype(np.float32).astype(dtype).astype(np.float64)
    return np.moveaxis((codes * scale).reshape(v.shape), -1, axis)


WIDE = False


def mx_kscale(k):
    if not WIDE:
        return np.ones(k)
    levels = np.array([10, -10, 5, -5, 0])
    a = np.random.permutation(np.resize(levels, k // 512 * 4)).reshape(k // 512, 4)
    idx = np.arange(k)
    return np.exp2(a[idx // 512, idx % 128 // 32])


BF16 = ml_dtypes.bfloat16


def bf(x):
    return np.asarray(x, np.float32).astype(BF16)


def f64(x):
    return np.asarray(x).astype(np.float64)


B, T, C, HQ, HKV, HD = 4, 1024, 1024, 4, 4, 128
E = HQ * HD


def sigmoid(v):
    return 1.0 / (1.0 + np.exp(-v))


def setup_inputs():
    t = mx_kscale(E)
    return {"attn": bf(np.random.standard_normal((B, T, HQ, HD)) * 0.5 * t.reshape(HQ, HD)),
            "Wg": bf(np.random.standard_normal((HD, HD)) * 2.0 / np.sqrt(HD) / t.max()),
            "bg": bf(np.random.standard_normal(HD) * 0.3),
            "Wo": bf(np.random.standard_normal((C, E)) * 2.0 / np.sqrt(E) / t),
            "bo": bf(np.random.standard_normal(C) * 0.1)}


def reference(attn, Wg, bg, Wo, bo):
    a = f64(attn)
    gate = sigmoid(a @ f64(Wg).T + f64(bg))
    h = (a * gate).reshape(B * T, E)
    return ((mxq(h, 1, "e4m3") @ mxq(f64(Wo), 1, "e4m3").T) + f64(bo)).reshape(B, T, C)

@@ -1,0 +1,222 @@
+from contextlib import ExitStack
+
+import concourse.mybir as mybir
+from concourse.masks import make_identity
+
+BF16 = mybir.dt.bfloat16
+F32 = mybir.dt.float32
+U32 = mybir.dt.uint32
+U8 = mybir.dt.uint8
+FP8X4 = mybir.dt.float8_e4m3fn_x4
+SIGMOID = mybir.ActivationFunctionType.Sigmoid
+MULT = mybir.AluOpType.mult
+ADD = mybir.AluOpType.add
+
+P = 128
+TOKENS = 4 * 1024
+HEADS = 4
+FEATURES = 128
+K = HEADS * FEATURES
+C_OUT = 1024
+BANK_F32 = 512
+C_HALVES = C_OUT // BANK_F32
+
+UNIT = 128
+UNITS_PER_PAIR = 2
+PAIRS_PER_GROUP = 2
+UNITS_PER_GROUP = UNITS_PER_PAIR * PAIRS_PER_GROUP
+N_UNITS = TOKENS // UNIT
+N_GROUPS = N_UNITS // UNITS_PER_GROUP
+
+LEAD_TRANSPOSE = 6
+LEAD_GATE = 4
+LEAD_QUANTISE = 2
+
+FLOPS = 2 * TOKENS * HEADS * FEATURES * FEATURES + 2 * TOKENS * K * C_OUT
+
+
+def tile_gqaselfattention_pb_t_kernel(tc, attn, Wg, bg, Wo, bo, out):
+    nc = tc.nc
+
+    attn_groups = attn.rearrange("b s h d -> (b s) (h d)").rearrange(
+        "(g q j) k -> g q j k", q=P, j=UNITS_PER_GROUP
+    )
+    out_groups = out.rearrange("b s c -> (b s) c").rearrange(
+        "(g q j) c -> g q j c", q=P, j=UNITS_PER_GROUP
+    )
+
+    with ExitStack() as ctx:
+        const = ctx.enter_context(tc.tile_pool(name="const", bufs=1))
+        attn_pool = ctx.enter_context(tc.tile_pool(name="attn", bufs=N_GROUPS))
+        at_pool = ctx.enter_context(tc.tile_pool(name="attn_t", bufs=6))
+        gate_pool = ctx.enter_context(tc.tile_pool(name="gate", bufs=4))
+        h_pool = ctx.enter_context(tc.tile_pool(name="h", bufs=4))
+        mx_pool = ctx.enter_context(tc.tile_pool(name="h_mx", bufs=6))
+        out_pool = ctx.enter_context(tc.tile_pool(name="out", bufs=6))
+        psum = ctx.enter_context(tc.psum_pool(name="psum", bufs=1))
+        ctx.enter_context(tc.manual_schedule())
+
+        ident = const.tile([P, P], BF16)
+        make_identity(nc, ident[:])
+        ones = const.tile([P, P], BF16)
+        nc.vector.memset(ones[:], 1.0)
+        vec_rows = const.tile([P, C_OUT + FEATURES], BF16)
+        nc.vector.memset(vec_rows[:], 0.0)
+
+        nc.scalar.dma_start(out=vec_rows[0:1, C_OUT : C_OUT + FEATURES], in_=bg.unsqueeze(0))
+        nc.scalar.dma_start(out=vec_rows[0:1, 0:C_OUT], in_=bo.unsqueeze(0))
+        warm = const.tile([P, 1], F32)
+        nc.scalar.activation(out=warm[:], in_=ones[:, 0:1], func=SIGMOID)
+        wg_sb = const.tile([P, FEATURES], BF16)
+        nc.sync.dma_start(out=wg_sb[:], in_=Wg)
+        attn_sb = []
+        wo_sb = []
+        for g in range(N_GROUPS):
+            attn_g = attn_pool.tile([P, UNITS_PER_GROUP, K], BF16)
+            nc.sync.dma_start(out=attn_g[:], in_=attn_groups[g])
+            attn_sb.append(attn_g)
+            if g == 0:
+                for half in range(C_HALVES):
+                    wo_half = const.tile([P, BANK_F32 // P, K], BF16, name="wo_half%d" % half)
+                    nc.sync.dma_start(
+                        out=wo_half[:],
+                        in_=Wo[half * BANK_F32 : (half + 1) * BANK_F32, :].rearrange(
+                            "(r p) k -> p r k", p=P
+                        ),
+                    )
+                    wo_sb.append(wo_half)
+
+        small_ps = psum.tile([P, 2, P], BF16, tag="z", bufs=2)
+        nc.tensor.transpose(out=small_ps[:, 0, :], in_=wg_sb[:], identity=ident[:])
+        nc.tensor.transpose(
+            out=small_ps[:, 1, :], in_=vec_rows[:, C_OUT : C_OUT + FEATURES], identity=ident[:]
+        )
+        wg_t = const.tile([P, FEATURES], BF16)
+        nc.vector.tensor_copy(out=wg_t[:], in_=small_ps[:, 0, :])
+        bg_col = const.tile([P, 1], F32)
+        nc.vector.tensor_copy(out=bg_col[:], in_=small_ps[:, 1, 0:1])
+
+        bo_all = const.tile([P, C_OUT], F32)
+        for half in range(C_HALVES):
+            cols = slice(half * BANK_F32, (half + 1) * BANK_F32)
+            bo_ps = psum.tile([P, BANK_F32], F32, tag="z", bufs=2)
+            nc.tensor.matmul(out=bo_ps[:], lhsT=ones[:], rhs=vec_rows[:, cols], start=True, stop=True)
+            nc.vector.tensor_copy(out=bo_all[:, cols], in_=bo_ps[:])
+
+        wo_words = const.tile([P, C_OUT], U32, align_bytes=64)
+        wo_scales = const.tile([P, C_OUT], U8, align_bytes=64)
+
+        def quantise_wo_half(half):
+            rows_per_bank = 2 * P
+            wo_grouped = const.tile(
+                [P, BANK_F32, HEADS], BF16, align_bytes=64, name="wo_grouped%d" % half
+            )
+            for b in range(BANK_F32 // rows_per_bank):
+                wo_t = psum.tile([P, HEADS, rows_per_bank], BF16, tag="acc", bufs=4)
+                for r in range(rows_per_bank // P):
+                    for t in range(HEADS):
+                        nc.tensor.transpose(
+                            out=wo_t[:, t, r * P : (r + 1) * P],
+                            in_=wo_sb[half][:, b * 2 + r, t * FEATURES : (t + 1) * FEATURES],
+                            identity=ident[:],
+                        )
+                grouped_cols = wo_grouped[:, b * rows_per_bank : (b + 1) * rows_per_bank, :]
+                if b % 2 == 0:
+                    nc.vector.tensor_copy(out=grouped_cols, in_=wo_t[:].rearrange("p t c -> p c t"))
+                else:
+                    nc.scalar.copy(out=grouped_cols, in_=wo_t[:].rearrange("p t c -> p c t"))
+            cols = slice(half * BANK_F32, (half + 1) * BANK_F32)
+            nc.vector.quantize_mx(
+                out=wo_words[:, cols].bitcast(FP8X4),
+                scales=wo_scales[:, cols],
+                in_=wo_grouped[:].rearrange("p c t -> p (c t)"),
+            )
+
+        attn_t = {}
+        h_tiles = {}
+        h_mx = {}
+
+        def transpose_pair(g, pair):
+            at_ps = psum.tile([P, UNITS_PER_PAIR, HEADS, UNIT], BF16, tag="tr", bufs=2)
+            for i in range(UNITS_PER_PAIR):
+                for t in range(HEADS):
+                    nc.tensor.transpose(
+                        out=at_ps[:, i, t, :],
+                        in_=attn_sb[g][
+                            :, pair * UNITS_PER_PAIR + i, t * FEATURES : (t + 1) * FEATURES
+                        ],
+                        identity=ident[:],
+                    )
+            at_sb = at_pool.tile([P, UNITS_PER_PAIR, HEADS, UNIT], BF16)
+            nc.scalar.copy(out=at_sb[:], in_=at_ps[:])
+            attn_t[(g, pair)] = at_sb
+
+        def gate_unit(u):
+            pair_key = (u // UNITS_PER_GROUP, (u % UNITS_PER_GROUP) // UNITS_PER_PAIR)
+            at_unit = attn_t[pair_key][:, u % UNITS_PER_PAIR]
+            z = psum.tile([P, HEADS, UNIT], F32, tag="z", bufs=2)
+            nc.tensor.matmul(
+                out=z[:].rearrange("p t q -> p (t q)"),
+                lhsT=wg_t[:],
+                rhs=at_unit.rearrange("p t q -> p (t q)"),
+                start=True,
+                stop=True,
+            )
+            gate = gate_pool.tile([P, UNIT, HEADS], F32)
+            nc.scalar.activation(
+                out=gate[:], in_=z[:].rearrange("p t q -> p q t"), func=SIGMOID, bias=bg_col[:, 0:1]
+            )
+            h = h_pool.tile([P, UNIT, HEADS], BF16, align_bytes=64)
+            nc.gpsimd.tensor_tensor(
+                out=h[:], in0=gate[:], in1=at_unit.rearrange("p t q -> p q t"), op=MULT
+            )
+            h_tiles[u] = h
+
+        def quantise_unit(u):
+            words = mx_pool.tile([P, UNIT], U32, align_bytes=64)
+            scales = mx_pool.tile([P, UNIT], U8, align_bytes=64)
+            nc.vector.quantize_mx(
+                out=words[:].bitcast(FP8X4),
+                scales=scales[:],
+                in_=h_tiles[u][:].rearrange("p q t -> p (q t)"),
+            )
+            h_mx[u] = (words, scales)
+
+        def project_unit(u):
+            out_sb = out_pool.tile([P, C_OUT], F32)
+            words, scales = h_mx[u]
+            for half in range(C_HALVES):
+                cols = slice(half * BANK_F32, (half + 1) * BANK_F32)
+                acc = psum.tile([P, BANK_F32], F32, tag="acc", bufs=4)
+                nc.tensor.matmul_mx(
+                    out=acc[:],
+                    lhsT=words[:].bitcast(FP8X4),
+                    lhsT_scale=scales[:],
+                    rhs=wo_words[:, cols].bitcast(FP8X4),
+                    rhs_scale=wo_scales[:, cols],
+                    start=True,
+                    stop=True,
+                )
+                nc.vector.tensor_tensor(out=out_sb[:, cols], in0=acc[:], in1=bo_all[:, cols], op=ADD)
+            nc.sync.dma_start(
+                out=out_groups[u // UNITS_PER_GROUP][:, u % UNITS_PER_GROUP, :], in_=out_sb[:]
+            )
+
+        for pair in range(PAIRS_PER_GROUP):
+            transpose_pair(0, pair)
+            quantise_wo_half(pair)
+            gate_unit(pair * UNITS_PER_PAIR)
+            gate_unit(pair * UNITS_PER_PAIR + 1)
+            quantise_unit(pair)
+        for pair in range(PAIRS_PER_GROUP):
+            transpose_pair(1, pair)
+        for u in range(N_UNITS):
+            project_unit(u)
+            u_transpose = u + LEAD_TRANSPOSE
+            if u_transpose % UNITS_PER_GROUP == 0 and u_transpose < N_UNITS:
+                for pair in range(PAIRS_PER_GROUP):
+                    transpose_pair(u_transpose // UNITS_PER_GROUP, pair)
+            if u + LEAD_GATE < N_UNITS:
+                gate_unit(u + LEAD_GATE)
+            if u + LEAD_QUANTISE < N_UNITS:
+                quantise_unit(u + LEAD_QUANTISE)

@@ -22,15 +22,9 @@ BANK_F32 = 512
 C_HALVES = C_OUT // BANK_F32
 
 UNIT = 128
-UNITS_PER_PAIR = 2
-PAIRS_PER_GROUP = 2
-UNITS_PER_GROUP = UNITS_PER_PAIR * PAIRS_PER_GROUP
-N_UNITS = TOKENS // UNIT
-N_GROUPS = N_UNITS // UNITS_PER_GROUP
-
-LEAD_TRANSPOSE = 6
-LEAD_GATE = 4
-LEAD_QUANTISE = 2
+UNITS = 4
+PAIR = 2
+N_GROUPS = TOKENS // (UNIT * UNITS)
 
 FLOPS = 2 * TOKENS * HEADS * FEATURES * FEATURES + 2 * TOKENS * K * C_OUT
 
@@ -39,52 +33,49 @@ def tile_gqaselfattention_pb_t_kernel(tc, attn, Wg, bg, Wo, bo, out):
     nc = tc.nc
 
     attn_groups = attn.rearrange("b s h d -> (b s) (h d)").rearrange(
-        "(g q j) k -> g q j k", q=P, j=UNITS_PER_GROUP
+        "(g q j) k -> g q j k", q=P, j=UNITS
     )
-    out_groups = out.rearrange("b s c -> (b s) c").rearrange(
-        "(g q j) c -> g q j c", q=P, j=UNITS_PER_GROUP
-    )
+    out_groups = out.rearrange("b s c -> (b s) c").rearrange("(g q j) c -> g q j c", q=P, j=UNITS)
 
     with ExitStack() as ctx:
         const = ctx.enter_context(tc.tile_pool(name="const", bufs=1))
         attn_pool = ctx.enter_context(tc.tile_pool(name="attn", bufs=N_GROUPS))
-        at_pool = ctx.enter_context(tc.tile_pool(name="attn_t", bufs=6))
-        gate_pool = ctx.enter_context(tc.tile_pool(name="gate", bufs=4))
-        h_pool = ctx.enter_context(tc.tile_pool(name="h", bufs=4))
-        mx_pool = ctx.enter_context(tc.tile_pool(name="h_mx", bufs=6))
+        at_pool = ctx.enter_context(tc.tile_pool(name="attn_t", bufs=3))
+        gate_pool = ctx.enter_context(tc.tile_pool(name="gate", bufs=3))
+        h_pool = ctx.enter_context(tc.tile_pool(name="h", bufs=1))
+        mx_pool = ctx.enter_context(tc.tile_pool(name="h_mx", bufs=2))
         out_pool = ctx.enter_context(tc.tile_pool(name="out", bufs=6))
         psum = ctx.enter_context(tc.psum_pool(name="psum", bufs=1))
         ctx.enter_context(tc.manual_schedule())
 
         ident = const.tile([P, P], BF16)
         make_identity(nc, ident[:])
-        ones = const.tile([P, P], BF16)
-        nc.vector.memset(ones[:], 1.0)
         vec_rows = const.tile([P, C_OUT + FEATURES], BF16)
         nc.vector.memset(vec_rows[:], 0.0)
-
-        nc.scalar.dma_start(out=vec_rows[0:1, C_OUT : C_OUT + FEATURES], in_=bg.unsqueeze(0))
-        nc.scalar.dma_start(out=vec_rows[0:1, 0:C_OUT], in_=bo.unsqueeze(0))
+        ones = const.tile([P, P], BF16)
+        nc.vector.memset(ones[:], 1.0)
         warm = const.tile([P, 1], F32)
         nc.scalar.activation(out=warm[:], in_=ones[:, 0:1], func=SIGMOID)
+
         wg_sb = const.tile([P, FEATURES], BF16)
         nc.sync.dma_start(out=wg_sb[:], in_=Wg)
         attn_sb = []
-        wo_sb = []
         for g in range(N_GROUPS):
-            attn_g = attn_pool.tile([P, UNITS_PER_GROUP, K], BF16)
-            nc.sync.dma_start(out=attn_g[:], in_=attn_groups[g])
+            attn_g = attn_pool.tile([P, UNITS, K], BF16)
             attn_sb.append(attn_g)
-            if g == 0:
-                for half in range(C_HALVES):
-                    wo_half = const.tile([P, BANK_F32 // P, K], BF16, name="wo_half%d" % half)
-                    nc.sync.dma_start(
-                        out=wo_half[:],
-                        in_=Wo[half * BANK_F32 : (half + 1) * BANK_F32, :].rearrange(
-                            "(r p) k -> p r k", p=P
-                        ),
-                    )
-                    wo_sb.append(wo_half)
+        nc.sync.dma_start(out=attn_sb[0][:], in_=attn_groups[0])
+        nc.sync.dma_start(out=vec_rows[0:1, C_OUT : C_OUT + FEATURES], in_=bg.unsqueeze(0))
+        nc.sync.dma_start(out=vec_rows[0:1, 0:C_OUT], in_=bo.unsqueeze(0))
+        wo_sb = []
+        for half in range(C_HALVES):
+            wo_half = const.tile([P, BANK_F32 // P, K], BF16, name="wo_half%d" % half)
+            nc.sync.dma_start(
+                out=wo_half[:],
+                in_=Wo[half * BANK_F32 : (half + 1) * BANK_F32, :].rearrange("(r p) k -> p r k", p=P),
+            )
+            wo_sb.append(wo_half)
+        for g in range(1, N_GROUPS):
+            nc.sync.dma_start(out=attn_sb[g][:], in_=attn_groups[g])
 
         small_ps = psum.tile([P, 2, P], BF16, tag="z", bufs=2)
         nc.tensor.transpose(out=small_ps[:, 0, :], in_=wg_sb[:], identity=ident[:])
@@ -97,11 +88,15 @@ def tile_gqaselfattention_pb_t_kernel(tc, attn, Wg, bg, Wo, bo, out):
         nc.vector.tensor_copy(out=bg_col[:], in_=small_ps[:, 1, 0:1])
 
         bo_all = const.tile([P, C_OUT], F32)
-        for half in range(C_HALVES):
-            cols = slice(half * BANK_F32, (half + 1) * BANK_F32)
-            bo_ps = psum.tile([P, BANK_F32], F32, tag="z", bufs=2)
-            nc.tensor.matmul(out=bo_ps[:], lhsT=ones[:], rhs=vec_rows[:, cols], start=True, stop=True)
-            nc.vector.tensor_copy(out=bo_all[:, cols], in_=bo_ps[:])
+
+        def spread_bo():
+            for half in range(C_HALVES):
+                cols = slice(half * BANK_F32, (half + 1) * BANK_F32)
+                bo_ps = psum.tile([P, BANK_F32], F32, tag="z", bufs=2)
+                nc.tensor.matmul(
+                    out=bo_ps[:], lhsT=ones[:], rhs=vec_rows[:, cols], start=True, stop=True
+                )
+                nc.vector.tensor_copy(out=bo_all[:, cols], in_=bo_ps[:])
 
         wo_words = const.tile([P, C_OUT], U32, align_bytes=64)
         wo_scales = const.tile([P, C_OUT], U8, align_bytes=64)
@@ -133,90 +128,106 @@ def tile_gqaselfattention_pb_t_kernel(tc, attn, Wg, bg, Wo, bo, out):
             )
 
         attn_t = {}
+        gates = {}
         h_tiles = {}
         h_mx = {}
 
-        def transpose_pair(g, pair):
-            at_ps = psum.tile([P, UNITS_PER_PAIR, HEADS, UNIT], BF16, tag="tr", bufs=2)
-            for i in range(UNITS_PER_PAIR):
-                for t in range(HEADS):
-                    nc.tensor.transpose(
-                        out=at_ps[:, i, t, :],
-                        in_=attn_sb[g][
-                            :, pair * UNITS_PER_PAIR + i, t * FEATURES : (t + 1) * FEATURES
-                        ],
-                        identity=ident[:],
-                    )
-            at_sb = at_pool.tile([P, UNITS_PER_PAIR, HEADS, UNIT], BF16)
-            nc.scalar.copy(out=at_sb[:], in_=at_ps[:])
-            attn_t[(g, pair)] = at_sb
+        def transpose_group(g):
+            at_sb = at_pool.tile([P, UNITS, HEADS, UNIT], BF16)
+            attn_t[g] = at_sb
+            for first in range(0, UNITS, PAIR):
+                at_ps = psum.tile([P, PAIR, HEADS, UNIT], BF16, tag="tr", bufs=2)
+                for i in range(PAIR):
+                    for t in range(HEADS):
+                        nc.tensor.transpose(
+                            out=at_ps[:, i, t, :],
+                            in_=attn_sb[g][:, first + i, t * FEATURES : (t + 1) * FEATURES],
+                            identity=ident[:],
+                        )
+                nc.scalar.copy(out=at_sb[:, first : first + PAIR], in_=at_ps[:])
 
-        def gate_unit(u):
-            pair_key = (u // UNITS_PER_GROUP, (u % UNITS_PER_GROUP) // UNITS_PER_PAIR)
-            at_unit = attn_t[pair_key][:, u % UNITS_PER_PAIR]
+        def gate_unit(g, j):
+            if j == 0:
+                gate_g = gate_pool.tile([P, UNITS, UNIT, HEADS], F32)
+                gates[g] = gate_g
             z = psum.tile([P, HEADS, UNIT], F32, tag="z", bufs=2)
             nc.tensor.matmul(
                 out=z[:].rearrange("p t q -> p (t q)"),
                 lhsT=wg_t[:],
-                rhs=at_unit.rearrange("p t q -> p (t q)"),
+                rhs=attn_t[g][:, j].rearrange("p t q -> p (t q)"),
                 start=True,
                 stop=True,
             )
-            gate = gate_pool.tile([P, UNIT, HEADS], F32)
             nc.scalar.activation(
-                out=gate[:], in_=z[:].rearrange("p t q -> p q t"), func=SIGMOID, bias=bg_col[:, 0:1]
+                out=gates[g][:, j],
+                in_=z[:].rearrange("p t q -> p q t"),
+                func=SIGMOID,
+                bias=bg_col[:, 0:1],
             )
-            h = h_pool.tile([P, UNIT, HEADS], BF16, align_bytes=64)
-            nc.gpsimd.tensor_tensor(
-                out=h[:], in0=gate[:], in1=at_unit.rearrange("p t q -> p q t"), op=MULT
-            )
-            h_tiles[u] = h
 
-        def quantise_unit(u):
-            words = mx_pool.tile([P, UNIT], U32, align_bytes=64)
-            scales = mx_pool.tile([P, UNIT], U8, align_bytes=64)
+        def multiply_group(engine, g):
+            h = h_pool.tile([P, UNITS, UNIT, HEADS], BF16, align_bytes=64)
+            engine.tensor_tensor(
+                out=h[:], in0=gates[g][:], in1=attn_t[g][:].rearrange("p j t q -> p j q t"), op=MULT
+            )
+            h_tiles[g] = h
+
+        def quantise_group(g):
+            words = mx_pool.tile([P, UNITS * UNIT], U32, align_bytes=64)
+            scales = mx_pool.tile([P, UNITS * UNIT], U8, align_bytes=64)
             nc.vector.quantize_mx(
                 out=words[:].bitcast(FP8X4),
                 scales=scales[:],
-                in_=h_tiles[u][:].rearrange("p q t -> p (q t)"),
+                in_=h_tiles[g][:].rearrange("p j q t -> p (j q t)"),
             )
-            h_mx[u] = (words, scales)
+            h_mx[g] = (words, scales)
 
-        def project_unit(u):
+        def project_unit(g, j):
             out_sb = out_pool.tile([P, C_OUT], F32)
-            words, scales = h_mx[u]
+            words, scales = h_mx[g]
+            tokens = slice(j * UNIT, (j + 1) * UNIT)
             for half in range(C_HALVES):
                 cols = slice(half * BANK_F32, (half + 1) * BANK_F32)
                 acc = psum.tile([P, BANK_F32], F32, tag="acc", bufs=4)
                 nc.tensor.matmul_mx(
                     out=acc[:],
-                    lhsT=words[:].bitcast(FP8X4),
-                    lhsT_scale=scales[:],
+                    lhsT=words[:, tokens].bitcast(FP8X4),
+                    lhsT_scale=scales[:, tokens],
                     rhs=wo_words[:, cols].bitcast(FP8X4),
                     rhs_scale=wo_scales[:, cols],
                     start=True,
                     stop=True,
                 )
                 nc.vector.tensor_tensor(out=out_sb[:, cols], in0=acc[:], in1=bo_all[:, cols], op=ADD)
-            nc.sync.dma_start(
-                out=out_groups[u // UNITS_PER_GROUP][:, u % UNITS_PER_GROUP, :], in_=out_sb[:]
-            )
+            nc.sync.dma_start(out=out_groups[g][:, j, :], in_=out_sb[:])
 
-        for pair in range(PAIRS_PER_GROUP):
-            transpose_pair(0, pair)
-            quantise_wo_half(pair)
-            gate_unit(pair * UNITS_PER_PAIR)
-            gate_unit(pair * UNITS_PER_PAIR + 1)
-            quantise_unit(pair)
-        for pair in range(PAIRS_PER_GROUP):
-            transpose_pair(1, pair)
-        for u in range(N_UNITS):
-            project_unit(u)
-            u_transpose = u + LEAD_TRANSPOSE
-            if u_transpose % UNITS_PER_GROUP == 0 and u_transpose < N_UNITS:
-                for pair in range(PAIRS_PER_GROUP):
-                    transpose_pair(u_transpose // UNITS_PER_GROUP, pair)
-            if u + LEAD_GATE < N_UNITS:
-                gate_unit(u + LEAD_GATE)
-            if u + LEAD_QUANTISE < N_UNITS:
-                quantise_unit(u + LEAD_QUANTISE)
+        transpose_group(0)
+        gate_unit(0, 0)
+        gate_unit(0, 1)
+        quantise_wo_half(0)
+        gate_unit(0, 2)
+        gate_unit(0, 3)
+        multiply_group(nc.vector, 0)
+        transpose_group(1)
+        gate_unit(1, 0)
+        gate_unit(1, 1)
+        quantise_wo_half(1)
+        gate_unit(1, 2)
+        gate_unit(1, 3)
+        quantise_group(0)
+        multiply_group(nc.gpsimd, 1)
+        spread_bo()
+
+        for g in range(N_GROUPS):
+            for j in range(UNITS):
+                project_unit(g, j)
+                if g + 2 < N_GROUPS:
+                    if j == 0:
+                        transpose_group(g + 2)
+                    if j == 1 or j == 2:
+                        gate_unit(g + 2, 2 * j - 2)
+                        gate_unit(g + 2, 2 * j - 1)
+                if j == 2 and g + 1 < N_GROUPS:
+                    quantise_group(g + 1)
+                    if g + 2 < N_GROUPS:
+                        multiply_group(nc.gpsimd, g + 2)

@@ -19,12 +19,17 @@ FEATURES = 128
 K = HEADS * FEATURES
 C_OUT = 1024
 BANK_F32 = 512
+BANK_BF16 = 2 * BANK_F32
 C_HALVES = C_OUT // BANK_F32
 
 UNIT = 128
 UNITS = 4
 PAIR = 2
 N_GROUPS = TOKENS // (UNIT * UNITS)
+VECTOR_UNITS = 1
+
+WO_BLOCKS = BANK_F32 * HEADS // P
+BLOCKS_PER_BANK = BANK_BF16 // P
 
 FLOPS = 2 * TOKENS * HEADS * FEATURES * FEATURES + 2 * TOKENS * K * C_OUT
 
@@ -36,6 +41,7 @@ def tile_gqaselfattention_pb_t_kernel(tc, attn, Wg, bg, Wo, bo, out):
         "(g q j) k -> g q j k", q=P, j=UNITS
     )
     out_groups = out.rearrange("b s c -> (b s) c").rearrange("(g q j) c -> g q j c", q=P, j=UNITS)
+    wo_rows = Wo.rearrange("c (t f) -> (c t) f", f=FEATURES)
 
     with ExitStack() as ctx:
         const = ctx.enter_context(tc.tile_pool(name="const", bufs=1))
@@ -48,34 +54,34 @@ def tile_gqaselfattention_pb_t_kernel(tc, attn, Wg, bg, Wo, bo, out):
         psum = ctx.enter_context(tc.psum_pool(name="psum", bufs=1))
         ctx.enter_context(tc.manual_schedule())
 
-        ident = const.tile([P, P], BF16)
-        make_identity(nc, ident[:])
         vec_rows = const.tile([P, C_OUT + FEATURES], BF16)
         nc.vector.memset(vec_rows[:], 0.0)
         ones = const.tile([P, P], BF16)
         nc.vector.memset(ones[:], 1.0)
+        ident = const.tile([P, P], BF16)
+        make_identity(nc, ident[:])
         warm = const.tile([P, 1], F32)
         nc.scalar.activation(out=warm[:], in_=ones[:, 0:1], func=SIGMOID)
 
         wg_sb = const.tile([P, FEATURES], BF16)
         nc.sync.dma_start(out=wg_sb[:], in_=Wg)
-        attn_sb = []
-        for g in range(N_GROUPS):
-            attn_g = attn_pool.tile([P, UNITS, K], BF16)
-            attn_sb.append(attn_g)
-        nc.sync.dma_start(out=attn_sb[0][:], in_=attn_groups[0])
         nc.sync.dma_start(out=vec_rows[0:1, C_OUT : C_OUT + FEATURES], in_=bg.unsqueeze(0))
         nc.sync.dma_start(out=vec_rows[0:1, 0:C_OUT], in_=bo.unsqueeze(0))
+        attn_sb = []
         wo_sb = []
-        for half in range(C_HALVES):
-            wo_half = const.tile([P, BANK_F32 // P, K], BF16, name="wo_half%d" % half)
-            nc.sync.dma_start(
-                out=wo_half[:],
-                in_=Wo[half * BANK_F32 : (half + 1) * BANK_F32, :].rearrange("(r p) k -> p r k", p=P),
-            )
-            wo_sb.append(wo_half)
-        for g in range(1, N_GROUPS):
-            nc.sync.dma_start(out=attn_sb[g][:], in_=attn_groups[g])
+        for g in range(N_GROUPS):
+            attn_g = attn_pool.tile([P, UNITS, K], BF16)
+            nc.sync.dma_start(out=attn_g[:], in_=attn_groups[g])
+            attn_sb.append(attn_g)
+            if g < C_HALVES:
+                wo_half = const.tile([P, WO_BLOCKS, FEATURES], BF16, name="wo_half%d" % g)
+                nc.sync.dma_start(
+                    out=wo_half[:],
+                    in_=wo_rows[g * WO_BLOCKS * P : (g + 1) * WO_BLOCKS * P, :].rearrange(
+                        "(b p) f -> p b f", p=P
+                    ),
+                )
+                wo_sb.append(wo_half)
 
         small_ps = psum.tile([P, 2, P], BF16, tag="z", bufs=2)
         nc.tensor.transpose(out=small_ps[:, 0, :], in_=wg_sb[:], identity=ident[:])
@@ -88,45 +94,41 @@ def tile_gqaselfattention_pb_t_kernel(tc, attn, Wg, bg, Wo, bo, out):
         nc.vector.tensor_copy(out=bg_col[:], in_=small_ps[:, 1, 0:1])
 
         bo_all = const.tile([P, C_OUT], F32)
-
-        def spread_bo():
-            for half in range(C_HALVES):
-                cols = slice(half * BANK_F32, (half + 1) * BANK_F32)
-                bo_ps = psum.tile([P, BANK_F32], F32, tag="z", bufs=2)
-                nc.tensor.matmul(
-                    out=bo_ps[:], lhsT=ones[:], rhs=vec_rows[:, cols], start=True, stop=True
-                )
-                nc.vector.tensor_copy(out=bo_all[:, cols], in_=bo_ps[:])
+        for half in range(C_HALVES):
+            cols = slice(half * BANK_F32, (half + 1) * BANK_F32)
+            bo_ps = psum.tile([P, BANK_F32], F32, tag="z", bufs=2)
+            nc.tensor.matmul(out=bo_ps[:], lhsT=ones[:], rhs=vec_rows[:, cols], start=True, stop=True)
+            nc.vector.tensor_copy(out=bo_all[:, cols], in_=bo_ps[:])
 
         wo_words = const.tile([P, C_OUT], U32, align_bytes=64)
         wo_scales = const.tile([P, C_OUT], U8, align_bytes=64)
+        wo_grouped = []
+        for half in range(C_HALVES):
+            grouped = const.tile([P, BANK_F32 * HEADS], BF16, align_bytes=64, name="wo_grouped%d" % half)
+            wo_grouped.append(grouped)
+
+        def transpose_wo_bank(half, bank):
+            wo_t = psum.tile([P, BLOCKS_PER_BANK, P], BF16, tag="acc", bufs=4)
+            for i in range(BLOCKS_PER_BANK):
+                nc.tensor.transpose(
+                    out=wo_t[:, i, :],
+                    in_=wo_sb[half][:, bank * BLOCKS_PER_BANK + i, :],
+                    identity=ident[:],
+                )
+            nc.vector.tensor_copy(
+                out=wo_grouped[half][:, bank * BANK_BF16 : (bank + 1) * BANK_BF16],
+                in_=wo_t[:].rearrange("p i c -> p (i c)"),
+            )
 
         def quantise_wo_half(half):
-            rows_per_bank = 2 * P
-            wo_grouped = const.tile(
-                [P, BANK_F32, HEADS], BF16, align_bytes=64, name="wo_grouped%d" % half
-            )
-            for b in range(BANK_F32 // rows_per_bank):
-                wo_t = psum.tile([P, HEADS, rows_per_bank], BF16, tag="acc", bufs=4)
-                for r in range(rows_per_bank // P):
-                    for t in range(HEADS):
-                        nc.tensor.transpose(
-                            out=wo_t[:, t, r * P : (r + 1) * P],
-                            in_=wo_sb[half][:, b * 2 + r, t * FEATURES : (t + 1) * FEATURES],
-                            identity=ident[:],
-                        )
-                grouped_cols = wo_grouped[:, b * rows_per_bank : (b + 1) * rows_per_bank, :]
-                if b % 2 == 0:
-                    nc.vector.tensor_copy(out=grouped_cols, in_=wo_t[:].rearrange("p t c -> p c t"))
-                else:
-                    nc.scalar.copy(out=grouped_cols, in_=wo_t[:].rearrange("p t c -> p c t"))
             cols = slice(half * BANK_F32, (half + 1) * BANK_F32)
             nc.vector.quantize_mx(
                 out=wo_words[:, cols].bitcast(FP8X4),
                 scales=wo_scales[:, cols],
-                in_=wo_grouped[:].rearrange("p c t -> p (c t)"),
+                in_=wo_grouped[half][:],
             )
 
+        attn_t_psum = {}
         attn_t = {}
         gates = {}
         h_tiles = {}
@@ -137,6 +139,8 @@ def tile_gqaselfattention_pb_t_kernel(tc, attn, Wg, bg, Wo, bo, out):
             attn_t[g] = at_sb
             for first in range(0, UNITS, PAIR):
                 at_ps = psum.tile([P, PAIR, HEADS, UNIT], BF16, tag="tr", bufs=2)
+                if first == 0:
+                    attn_t_psum[g] = at_ps
                 for i in range(PAIR):
                     for t in range(HEADS):
                         nc.tensor.transpose(
@@ -165,12 +169,24 @@ def tile_gqaselfattention_pb_t_kernel(tc, attn, Wg, bg, Wo, bo, out):
                 bias=bg_col[:, 0:1],
             )
 
-        def multiply_group(engine, g):
+        def new_h(g):
             h = h_pool.tile([P, UNITS, UNIT, HEADS], BF16, align_bytes=64)
-            engine.tensor_tensor(
-                out=h[:], in0=gates[g][:], in1=attn_t[g][:].rearrange("p j t q -> p j q t"), op=MULT
-            )
             h_tiles[g] = h
+
+        def multiply(engine, g, units, attn_t_units):
+            engine.tensor_tensor(
+                out=h_tiles[g][:, units],
+                in0=gates[g][:, units],
+                in1=attn_t_units.rearrange("p j t q -> p j q t"),
+                op=MULT,
+            )
+
+        def multiply_group(g):
+            new_h(g)
+            by_vector = slice(0, VECTOR_UNITS)
+            by_gpsimd = slice(VECTOR_UNITS, UNITS)
+            multiply(nc.vector, g, by_vector, attn_t_psum[g][:, by_vector])
+            multiply(nc.gpsimd, g, by_gpsimd, attn_t[g][:, by_gpsimd])
 
         def quantise_group(g):
             words = mx_pool.tile([P, UNITS * UNIT], U32, align_bytes=64)
@@ -201,22 +217,22 @@ def tile_gqaselfattention_pb_t_kernel(tc, attn, Wg, bg, Wo, bo, out):
                 nc.vector.tensor_tensor(out=out_sb[:, cols], in0=acc[:], in1=bo_all[:, cols], op=ADD)
             nc.sync.dma_start(out=out_groups[g][:, j, :], in_=out_sb[:])
 
-        transpose_group(0)
-        gate_unit(0, 0)
-        gate_unit(0, 1)
-        quantise_wo_half(0)
-        gate_unit(0, 2)
-        gate_unit(0, 3)
-        multiply_group(nc.vector, 0)
-        transpose_group(1)
-        gate_unit(1, 0)
-        gate_unit(1, 1)
-        quantise_wo_half(1)
-        gate_unit(1, 2)
-        gate_unit(1, 3)
+        def gates_and_wo_half(g):
+            transpose_group(g)
+            gate_unit(g, 0)
+            gate_unit(g, 1)
+            transpose_wo_bank(g, 0)
+            gate_unit(g, 2)
+            transpose_wo_bank(g, 1)
+            gate_unit(g, 3)
+            quantise_wo_half(g)
+
+        gates_and_wo_half(0)
+        new_h(0)
+        multiply(nc.vector, 0, slice(0, UNITS), attn_t[0][:])
         quantise_group(0)
-        multiply_group(nc.gpsimd, 1)
-        spread_bo()
+        gates_and_wo_half(1)
+        multiply_group(1)
 
         for g in range(N_GROUPS):
             for j in range(UNITS):
@@ -230,4 +246,4 @@ def tile_gqaselfattention_pb_t_kernel(tc, attn, Wg, bg, Wo, bo, out):
                 if j == 2 and g + 1 < N_GROUPS:
                     quantise_group(g + 1)
                     if g + 2 < N_GROUPS:
-                        multiply_group(nc.gpsimd, g + 2)
+                        multiply_group(g + 2)

@@ -215,7 +215,7 @@ def tile_gqaselfattention_pb_t_kernel(tc, attn, Wg, bg, Wo, bo, out):
                     stop=True,
                 )
                 nc.vector.tensor_tensor(out=out_sb[:, cols], in0=acc[:], in1=bo_all[:, cols], op=ADD)
-            nc.sync.dma_start(out=out_groups[g][:, j, :], in_=out_sb[:])
+                nc.sync.dma_start(out=out_groups[g][:, j, cols], in_=out_sb[:, cols])
 
         def gates_and_wo_half(g):
             transpose_group(g)
@@ -230,8 +230,8 @@ def tile_gqaselfattention_pb_t_kernel(tc, attn, Wg, bg, Wo, bo, out):
         gates_and_wo_half(0)
         new_h(0)
         multiply(nc.vector, 0, slice(0, UNITS), attn_t[0][:])
-        quantise_group(0)
         gates_and_wo_half(1)
+        quantise_group(0)
         multiply_group(1)
 
         for g in range(N_GROUPS):

@@ -215,7 +215,7 @@ def tile_gqaselfattention_pb_t_kernel(tc, attn, Wg, bg, Wo, bo, out):
                     stop=True,
                 )
                 nc.vector.tensor_tensor(out=out_sb[:, cols], in0=acc[:], in1=bo_all[:, cols], op=ADD)
-                nc.sync.dma_start(out=out_groups[g][:, j, cols], in_=out_sb[:, cols])
+            nc.sync.dma_start(out=out_groups[g][:, j, :], in_=out_sb[:])
 
         def gates_and_wo_half(g):
             transpose_group(g)

@@ -26,7 +26,8 @@ UNIT = 128
 UNITS = 4
 PAIR = 2
 N_GROUPS = TOKENS // (UNIT * UNITS)
-VECTOR_UNITS = 1
+VECTOR_TOKENS = 64
+WARM = 3
 
 WO_BLOCKS = BANK_F32 * HEADS // P
 BLOCKS_PER_BANK = BANK_BF16 // P
@@ -55,57 +56,70 @@ def tile_gqaselfattention_pb_t_kernel(tc, attn, Wg, bg, Wo, bo, out):
         ctx.enter_context(tc.manual_schedule())
 
         vec_rows = const.tile([P, C_OUT + FEATURES], BF16)
-        nc.vector.memset(vec_rows[:], 0.0)
-        ones = const.tile([P, P], BF16)
-        nc.vector.memset(ones[:], 1.0)
+        nc.vector.memset(vec_rows[:].bitcast(F32), 0.0)
+        warm_rows = const.tile([P, BANK_F32], BF16)
+        nc.vector.memset(warm_rows[:].bitcast(F32), 0.0)
         ident = const.tile([P, P], BF16)
         make_identity(nc, ident[:])
+        ones = const.tile([P, P], BF16)
+        nc.vector.memset(ones[:], 1.0)
         warm = const.tile([P, 1], F32)
         nc.scalar.activation(out=warm[:], in_=ones[:, 0:1], func=SIGMOID)
 
         wg_sb = const.tile([P, FEATURES], BF16)
-        nc.sync.dma_start(out=wg_sb[:], in_=Wg)
-        nc.sync.dma_start(out=vec_rows[0:1, C_OUT : C_OUT + FEATURES], in_=bg.unsqueeze(0))
-        nc.sync.dma_start(out=vec_rows[0:1, 0:C_OUT], in_=bo.unsqueeze(0))
         attn_sb = []
-        wo_sb = []
         for g in range(N_GROUPS):
             attn_g = attn_pool.tile([P, UNITS, K], BF16)
-            nc.sync.dma_start(out=attn_g[:], in_=attn_groups[g])
             attn_sb.append(attn_g)
-            if g < C_HALVES:
-                wo_half = const.tile([P, WO_BLOCKS, FEATURES], BF16, name="wo_half%d" % g)
-                nc.sync.dma_start(
-                    out=wo_half[:],
-                    in_=wo_rows[g * WO_BLOCKS * P : (g + 1) * WO_BLOCKS * P, :].rearrange(
-                        "(b p) f -> p b f", p=P
-                    ),
-                )
-                wo_sb.append(wo_half)
-
-        small_ps = psum.tile([P, 2, P], BF16, tag="z", bufs=2)
-        nc.tensor.transpose(out=small_ps[:, 0, :], in_=wg_sb[:], identity=ident[:])
-        nc.tensor.transpose(
-            out=small_ps[:, 1, :], in_=vec_rows[:, C_OUT : C_OUT + FEATURES], identity=ident[:]
-        )
-        wg_t = const.tile([P, FEATURES], BF16)
-        nc.vector.tensor_copy(out=wg_t[:], in_=small_ps[:, 0, :])
-        bg_col = const.tile([P, 1], F32)
-        nc.vector.tensor_copy(out=bg_col[:], in_=small_ps[:, 1, 0:1])
-
-        bo_all = const.tile([P, C_OUT], F32)
+        wo_sb = []
         for half in range(C_HALVES):
-            cols = slice(half * BANK_F32, (half + 1) * BANK_F32)
-            bo_ps = psum.tile([P, BANK_F32], F32, tag="z", bufs=2)
-            nc.tensor.matmul(out=bo_ps[:], lhsT=ones[:], rhs=vec_rows[:, cols], start=True, stop=True)
-            nc.vector.tensor_copy(out=bo_all[:, cols], in_=bo_ps[:])
+            wo_half = const.tile([P, WO_BLOCKS, FEATURES], BF16, name="wo_half%d" % half)
+            wo_sb.append(wo_half)
 
+        def load_units(g, first, count):
+            nc.sync.dma_start(
+                out=attn_sb[g][:, first : first + count], in_=attn_groups[g][:, first : first + count]
+            )
+
+        def load_wo_half(half):
+            nc.sync.dma_start(
+                out=wo_sb[half][:],
+                in_=wo_rows[half * WO_BLOCKS * P : (half + 1) * WO_BLOCKS * P, :].rearrange(
+                    "(b p) f -> p b f", p=P
+                ),
+            )
+
+        nc.sync.dma_start(out=wg_sb[:], in_=Wg)
+        load_units(0, 0, PAIR)
+        nc.sync.dma_start(out=vec_rows[0:1, 0:C_OUT], in_=bo.unsqueeze(0))
+        nc.sync.dma_start(out=vec_rows[0:1, C_OUT : C_OUT + FEATURES], in_=bg.unsqueeze(0))
+        load_units(0, PAIR, PAIR)
+        load_wo_half(0)
+        load_units(1, 0, UNITS)
+        load_wo_half(1)
+        for g in range(2, N_GROUPS):
+            load_units(g, 0, UNITS)
+
+        wg_t = const.tile([P, FEATURES], BF16)
+        bg_col = const.tile([P, 1], F32)
+        bo_all = const.tile([P, C_OUT], F32)
         wo_words = const.tile([P, C_OUT], U32, align_bytes=64)
         wo_scales = const.tile([P, C_OUT], U8, align_bytes=64)
         wo_grouped = []
         for half in range(C_HALVES):
             grouped = const.tile([P, BANK_F32 * HEADS], BF16, align_bytes=64, name="wo_grouped%d" % half)
             wo_grouped.append(grouped)
+        wo_t_psum = {}
+        attn_t_psum = {}
+        attn_t = {}
+        gates = {}
+        h_tiles = {}
+        h_mx = {}
+
+        def transpose_small(columns_of, name):
+            ps = psum.tile([P, P], BF16, tag="z", bufs=2, name=name)
+            nc.tensor.transpose(out=ps[:], in_=columns_of, identity=ident[:])
+            return ps
 
         def transpose_wo_bank(half, bank):
             wo_t = psum.tile([P, BLOCKS_PER_BANK, P], BF16, tag="acc", bufs=4)
@@ -115,9 +129,12 @@ def tile_gqaselfattention_pb_t_kernel(tc, attn, Wg, bg, Wo, bo, out):
                     in_=wo_sb[half][:, bank * BLOCKS_PER_BANK + i, :],
                     identity=ident[:],
                 )
-            nc.vector.tensor_copy(
+            wo_t_psum[half, bank] = wo_t
+
+        def copy_wo_bank(copy, half, bank):
+            copy(
                 out=wo_grouped[half][:, bank * BANK_BF16 : (bank + 1) * BANK_BF16],
-                in_=wo_t[:].rearrange("p i c -> p (i c)"),
+                in_=wo_t_psum[half, bank][:].rearrange("p i c -> p (i c)"),
             )
 
         def quantise_wo_half(half):
@@ -128,122 +145,213 @@ def tile_gqaselfattention_pb_t_kernel(tc, attn, Wg, bg, Wo, bo, out):
                 in_=wo_grouped[half][:],
             )
 
-        attn_t_psum = {}
-        attn_t = {}
-        gates = {}
-        h_tiles = {}
-        h_mx = {}
+        def transpose_units(g, first, count):
+            at_ps = psum.tile([P, HEADS, count, UNIT], BF16, tag="tr", bufs=2)
+            attn_t_psum[g, first] = at_ps
+            for i in range(count):
+                for t in range(HEADS):
+                    nc.tensor.transpose(
+                        out=at_ps[:, t, i, :],
+                        in_=attn_sb[g][:, first + i, t * FEATURES : (t + 1) * FEATURES],
+                        identity=ident[:],
+                    )
 
-        def transpose_group(g):
-            at_sb = at_pool.tile([P, UNITS, HEADS, UNIT], BF16)
-            attn_t[g] = at_sb
-            for first in range(0, UNITS, PAIR):
-                at_ps = psum.tile([P, PAIR, HEADS, UNIT], BF16, tag="tr", bufs=2)
-                if first == 0:
-                    attn_t_psum[g] = at_ps
-                for i in range(PAIR):
-                    for t in range(HEADS):
-                        nc.tensor.transpose(
-                            out=at_ps[:, i, t, :],
-                            in_=attn_sb[g][:, first + i, t * FEATURES : (t + 1) * FEATURES],
-                            identity=ident[:],
-                        )
-                nc.scalar.copy(out=at_sb[:, first : first + PAIR], in_=at_ps[:])
+        def copy_units(copy, g, first, count):
+            if first == 0:
+                at_sb = at_pool.tile([P, UNITS * UNIT, HEADS], BF16)
+                attn_t[g] = at_sb
+            copy(
+                out=attn_t[g][:, first * UNIT : (first + count) * UNIT],
+                in_=attn_t_psum[g, first][:].rearrange("p t i q -> p (i q) t"),
+            )
 
         def gate_unit(g, j):
             if j == 0:
-                gate_g = gate_pool.tile([P, UNITS, UNIT, HEADS], F32)
+                gate_g = gate_pool.tile([P, UNITS * UNIT, HEADS], F32)
                 gates[g] = gate_g
-            z = psum.tile([P, HEADS, UNIT], F32, tag="z", bufs=2)
+            tokens = slice(j * UNIT, (j + 1) * UNIT)
+            z = psum.tile([P, UNIT * HEADS], F32, tag="z", bufs=2)
             nc.tensor.matmul(
-                out=z[:].rearrange("p t q -> p (t q)"),
+                out=z[:],
                 lhsT=wg_t[:],
-                rhs=attn_t[g][:, j].rearrange("p t q -> p (t q)"),
+                rhs=attn_t[g][:, tokens].rearrange("p q t -> p (q t)"),
                 start=True,
                 stop=True,
             )
             nc.scalar.activation(
-                out=gates[g][:, j],
-                in_=z[:].rearrange("p t q -> p q t"),
+                out=gates[g][:, tokens].rearrange("p q t -> p (q t)"),
+                in_=z[:],
                 func=SIGMOID,
                 bias=bg_col[:, 0:1],
             )
 
         def new_h(g):
-            h = h_pool.tile([P, UNITS, UNIT, HEADS], BF16, align_bytes=64)
+            h = h_pool.tile([P, UNITS * UNIT, HEADS], BF16, align_bytes=64)
             h_tiles[g] = h
 
-        def multiply(engine, g, units, attn_t_units):
+        def multiply(engine, g, tokens, attn_t_tokens):
             engine.tensor_tensor(
-                out=h_tiles[g][:, units],
-                in0=gates[g][:, units],
-                in1=attn_t_units.rearrange("p j t q -> p j q t"),
+                out=h_tiles[g][:, tokens],
+                in0=gates[g][:, tokens],
+                in1=attn_t_tokens,
                 op=MULT,
             )
 
+        def multiply_sbuf(engine, g, first_token, last_token):
+            tokens = slice(first_token, last_token)
+            multiply(engine, g, tokens, attn_t[g][:, tokens])
+
         def multiply_group(g):
+            by_vector = VECTOR_TOKENS
+            n = UNITS * UNIT - by_vector
             new_h(g)
-            by_vector = slice(0, VECTOR_UNITS)
-            by_gpsimd = slice(VECTOR_UNITS, UNITS)
-            multiply(nc.vector, g, by_vector, attn_t_psum[g][:, by_vector])
-            multiply(nc.gpsimd, g, by_gpsimd, attn_t[g][:, by_gpsimd])
+            multiply_sbuf(nc.gpsimd, g, 0, PAIR * UNIT)
+            multiply_sbuf(nc.gpsimd, g, PAIR * UNIT, n)
 
-        def quantise_group(g):
-            words = mx_pool.tile([P, UNITS * UNIT], U32, align_bytes=64)
-            scales = mx_pool.tile([P, UNITS * UNIT], U8, align_bytes=64)
-            nc.vector.quantize_mx(
-                out=words[:].bitcast(FP8X4),
-                scales=scales[:],
-                in_=h_tiles[g][:].rearrange("p j q t -> p (j q t)"),
+        def multiply_rest(g):
+            by_vector = VECTOR_TOKENS
+            n = UNITS * UNIT - by_vector
+            multiply(
+                nc.vector,
+                g,
+                slice(n, UNITS * UNIT),
+                attn_t_psum[g, PAIR][:].rearrange("p t i q -> p (i q) t")[:, PAIR * UNIT - by_vector :],
             )
-            h_mx[g] = (words, scales)
 
-        def project_unit(g, j):
-            out_sb = out_pool.tile([P, C_OUT], F32)
+        def quantise_units(g, first, count):
+            if first == 0:
+                words = mx_pool.tile([P, UNITS * UNIT], U32, align_bytes=64)
+                scales = mx_pool.tile([P, UNITS * UNIT], U8, align_bytes=64)
+                h_mx[g] = (words, scales)
+            words, scales = h_mx[g]
+            tokens = slice(first * UNIT, (first + count) * UNIT)
+            nc.vector.quantize_mx(
+                out=words[:, tokens].bitcast(FP8X4),
+                scales=scales[:, tokens],
+                in_=h_tiles[g][:, tokens].rearrange("p q t -> p (q t)"),
+            )
+
+        out_tiles = {}
+
+        def project(g, j, half):
+            if (g, j) not in out_tiles:
+                out_sb = out_pool.tile([P, C_OUT], F32)
+                out_tiles[g, j] = out_sb
+            out_sb = out_tiles[g, j]
             words, scales = h_mx[g]
             tokens = slice(j * UNIT, (j + 1) * UNIT)
-            for half in range(C_HALVES):
-                cols = slice(half * BANK_F32, (half + 1) * BANK_F32)
-                acc = psum.tile([P, BANK_F32], F32, tag="acc", bufs=4)
-                nc.tensor.matmul_mx(
-                    out=acc[:],
-                    lhsT=words[:, tokens].bitcast(FP8X4),
-                    lhsT_scale=scales[:, tokens],
-                    rhs=wo_words[:, cols].bitcast(FP8X4),
-                    rhs_scale=wo_scales[:, cols],
-                    start=True,
-                    stop=True,
-                )
-                nc.vector.tensor_tensor(out=out_sb[:, cols], in0=acc[:], in1=bo_all[:, cols], op=ADD)
-            nc.sync.dma_start(out=out_groups[g][:, j, :], in_=out_sb[:])
+            cols = slice(half * BANK_F32, (half + 1) * BANK_F32)
+            acc = psum.tile([P, BANK_F32], F32, tag="acc", bufs=4)
+            nc.tensor.matmul_mx(
+                out=acc[:],
+                lhsT=words[:, tokens].bitcast(FP8X4),
+                lhsT_scale=scales[:, tokens],
+                rhs=wo_words[:, cols].bitcast(FP8X4),
+                rhs_scale=wo_scales[:, cols],
+                start=True,
+                stop=True,
+            )
+            nc.vector.tensor_tensor(out=out_sb[:, cols], in0=acc[:], in1=bo_all[:, cols], op=ADD)
 
-        def gates_and_wo_half(g):
-            transpose_group(g)
-            gate_unit(g, 0)
-            gate_unit(g, 1)
-            transpose_wo_bank(g, 0)
-            gate_unit(g, 2)
-            transpose_wo_bank(g, 1)
-            gate_unit(g, 3)
-            quantise_wo_half(g)
+        def store(g, j, cols=slice(0, C_OUT)):
+            nc.sync.dma_start(out=out_groups[g][:, j, cols], in_=out_tiles[g, j][:, cols])
 
-        gates_and_wo_half(0)
+        for i in range(WARM):
+            junk = psum.tile([P, BANK_F32], F32, tag="acc", bufs=4)
+            nc.tensor.matmul(out=junk[:], lhsT=warm_rows[:, 0:P], rhs=warm_rows[:], start=True, stop=True)
+        wg_ps = transpose_small(wg_sb[:], "wg_ps")
+        nc.vector.tensor_copy(out=wg_t[:], in_=wg_ps[:])
+        transpose_units(0, 0, 1)
+        copy_units(nc.scalar.copy, 0, 0, 1)
+        transpose_units(0, 1, 1)
+        copy_units(nc.vector.tensor_copy, 0, 1, 1)
+        for half, copy in enumerate((nc.scalar.copy, nc.vector.tensor_copy)):
+            cols = slice(half * BANK_F32, (half + 1) * BANK_F32)
+            bo_ps = psum.tile([P, BANK_F32], F32, tag="acc", bufs=4)
+            nc.tensor.matmul(out=bo_ps[:], lhsT=ones[:], rhs=vec_rows[:, cols], start=True, stop=True)
+            copy(out=bo_all[:, cols], in_=bo_ps[:])
+        bg_ps = transpose_small(vec_rows[:, C_OUT : C_OUT + FEATURES], "bg_ps")
+        nc.vector.tensor_copy(out=bg_col[:], in_=bg_ps[:, 0:1])
         new_h(0)
-        multiply(nc.vector, 0, slice(0, UNITS), attn_t[0][:])
-        gates_and_wo_half(1)
-        quantise_group(0)
+        gate_unit(0, 0)
+        gate_unit(0, 1)
+        transpose_units(0, 2, 1)
+        copy_units(nc.scalar.copy, 0, 2, 1)
+        transpose_units(0, 3, 1)
+        copy_units(nc.scalar.copy, 0, 3, 1)
+        multiply_sbuf(nc.vector, 0, 0, UNIT)
+        multiply_sbuf(nc.gpsimd, 0, UNIT, 2 * UNIT)
+        transpose_wo_bank(0, 0)
+        copy_wo_bank(nc.vector.tensor_copy, 0, 0)
+        transpose_wo_bank(0, 1)
+        copy_wo_bank(nc.vector.tensor_copy, 0, 1)
+        gate_unit(0, 2)
+        gate_unit(0, 3)
+        transpose_units(1, 0, PAIR)
+        copy_units(nc.scalar.copy, 1, 0, PAIR)
+        multiply_sbuf(nc.vector, 0, 2 * UNIT, 3 * UNIT)
+        quantise_wo_half(0)
+        quantise_units(0, 0, PAIR)
+        multiply_sbuf(nc.vector, 0, 3 * UNIT, 4 * UNIT)
+        transpose_units(1, PAIR, PAIR)
+        copy_units(nc.scalar.copy, 1, PAIR, PAIR)
+        project(0, 0, 0)
+        project(0, 1, 0)
+        quantise_units(0, PAIR, PAIR)
+        gate_unit(1, 0)
+        gate_unit(1, 1)
+        transpose_wo_bank(1, 0)
+        copy_wo_bank(nc.scalar.copy, 1, 0)
+        project(0, 2, 0)
+        transpose_wo_bank(1, 1)
+        copy_wo_bank(nc.vector.tensor_copy, 1, 1)
+        project(0, 3, 0)
+        gate_unit(1, 2)
+        gate_unit(1, 3)
+        quantise_wo_half(1)
         multiply_group(1)
+        transpose_units(2, 0, PAIR)
+        copy_units(nc.scalar.copy, 2, 0, PAIR)
+        transpose_units(2, PAIR, PAIR)
+        copy_units(nc.scalar.copy, 2, PAIR, PAIR)
+        project(0, 0, 1)
+        store(0, 0)
+        project(0, 1, 1)
+        store(0, 1)
+        multiply_rest(1)
+        gate_unit(2, 0)
+        gate_unit(2, 1)
+        project(0, 2, 1)
+        store(0, 2)
+        project(0, 3, 1)
+        store(0, 3)
+        quantise_units(1, 0, UNITS)
+        gate_unit(2, 2)
+        gate_unit(2, 3)
+        multiply_group(2)
 
-        for g in range(N_GROUPS):
+        for g in range(1, N_GROUPS):
+            ahead = g + 2
             for j in range(UNITS):
-                project_unit(g, j)
-                if g + 2 < N_GROUPS:
-                    if j == 0:
-                        transpose_group(g + 2)
-                    if j == 1 or j == 2:
-                        gate_unit(g + 2, 2 * j - 2)
-                        gate_unit(g + 2, 2 * j - 1)
-                if j == 2 and g + 1 < N_GROUPS:
-                    quantise_group(g + 1)
-                    if g + 2 < N_GROUPS:
-                        multiply_group(g + 2)
+                for half in range(C_HALVES):
+                    bank = j * C_HALVES + half
+                    project(g, j, half)
+                    last = g == N_GROUPS - 1 and j == UNITS - 1
+                    if last:
+                        store(g, j, slice(half * BANK_F32, (half + 1) * BANK_F32))
+                    elif half == C_HALVES - 1:
+                        store(g, j)
+                    if bank == 0 and g + 1 < N_GROUPS:
+                        multiply_rest(g + 1)
+                    if ahead < N_GROUPS:
+                        for first, when in ((0, 2), (PAIR, 3)):
+                            if bank == when:
+                                transpose_units(ahead, first, PAIR)
+                                copy_units(nc.scalar.copy, ahead, first, PAIR)
+                        for unit, when in enumerate((4, 5, 6, 7)):
+                            if bank == when:
+                                gate_unit(ahead, unit)
+                    if bank == 5 and g + 1 < N_GROUPS:
+                        quantise_units(g + 1, 0, UNITS)
+                    if bank == 7 and ahead < N_GROUPS:
+                        multiply_group(ahead)

@@ -90,9 +90,10 @@ def tile_gqaselfattention_pb_t_kernel(tc, attn, Wg, bg, Wo, bo, out):
             )
 
         nc.sync.dma_start(out=wg_sb[:], in_=Wg)
-        load_units(0, 0, PAIR)
-        nc.sync.dma_start(out=vec_rows[0:1, 0:C_OUT], in_=bo.unsqueeze(0))
+        load_units(0, 0, 1)
+        load_units(0, 1, 1)
         nc.sync.dma_start(out=vec_rows[0:1, C_OUT : C_OUT + FEATURES], in_=bg.unsqueeze(0))
+        nc.sync.dma_start(out=vec_rows[0:1, 0:C_OUT], in_=bo.unsqueeze(0))
         load_units(0, PAIR, PAIR)
         load_wo_half(0)
         load_units(1, 0, UNITS)
@@ -201,21 +202,18 @@ def tile_gqaselfattention_pb_t_kernel(tc, attn, Wg, bg, Wo, bo, out):
             tokens = slice(first_token, last_token)
             multiply(engine, g, tokens, attn_t[g][:, tokens])
 
-        def multiply_group(g):
-            by_vector = VECTOR_TOKENS
-            n = UNITS * UNIT - by_vector
+        def multiply_by_gpsimd(g, vector_tokens):
             new_h(g)
             multiply_sbuf(nc.gpsimd, g, 0, PAIR * UNIT)
-            multiply_sbuf(nc.gpsimd, g, PAIR * UNIT, n)
+            multiply_sbuf(nc.gpsimd, g, PAIR * UNIT, UNITS * UNIT - vector_tokens)
 
-        def multiply_rest(g):
-            by_vector = VECTOR_TOKENS
-            n = UNITS * UNIT - by_vector
+        def multiply_by_vector(g, vector_tokens):
+            attn_t_pair = attn_t_psum[g, PAIR][:].rearrange("p t i q -> p (i q) t")
             multiply(
                 nc.vector,
                 g,
-                slice(n, UNITS * UNIT),
-                attn_t_psum[g, PAIR][:].rearrange("p t i q -> p (i q) t")[:, PAIR * UNIT - by_vector :],
+                slice(UNITS * UNIT - vector_tokens, UNITS * UNIT),
+                attn_t_pair[:, PAIR * UNIT - vector_tokens :],
             )
 
         def quantise_units(g, first, count):
@@ -265,13 +263,13 @@ def tile_gqaselfattention_pb_t_kernel(tc, attn, Wg, bg, Wo, bo, out):
         copy_units(nc.scalar.copy, 0, 0, 1)
         transpose_units(0, 1, 1)
         copy_units(nc.vector.tensor_copy, 0, 1, 1)
+        bg_ps = transpose_small(vec_rows[:, C_OUT : C_OUT + FEATURES], "bg_ps")
+        nc.vector.tensor_copy(out=bg_col[:], in_=bg_ps[:, 0:1])
         for half, copy in enumerate((nc.scalar.copy, nc.vector.tensor_copy)):
             cols = slice(half * BANK_F32, (half + 1) * BANK_F32)
             bo_ps = psum.tile([P, BANK_F32], F32, tag="acc", bufs=4)
             nc.tensor.matmul(out=bo_ps[:], lhsT=ones[:], rhs=vec_rows[:, cols], start=True, stop=True)
             copy(out=bo_all[:, cols], in_=bo_ps[:])
-        bg_ps = transpose_small(vec_rows[:, C_OUT : C_OUT + FEATURES], "bg_ps")
-        nc.vector.tensor_copy(out=bg_col[:], in_=bg_ps[:, 0:1])
         new_h(0)
         gate_unit(0, 0)
         gate_unit(0, 1)
@@ -287,29 +285,29 @@ def tile_gqaselfattention_pb_t_kernel(tc, attn, Wg, bg, Wo, bo, out):
         copy_wo_bank(nc.vector.tensor_copy, 0, 1)
         gate_unit(0, 2)
         gate_unit(0, 3)
-        transpose_units(1, 0, PAIR)
-        copy_units(nc.scalar.copy, 1, 0, PAIR)
-        multiply_sbuf(nc.vector, 0, 2 * UNIT, 3 * UNIT)
         quantise_wo_half(0)
         quantise_units(0, 0, PAIR)
+        multiply_sbuf(nc.vector, 0, 2 * UNIT, 3 * UNIT)
         multiply_sbuf(nc.vector, 0, 3 * UNIT, 4 * UNIT)
+        quantise_units(0, PAIR, PAIR)
+        transpose_units(1, 0, PAIR)
+        copy_units(nc.scalar.copy, 1, 0, PAIR)
         transpose_units(1, PAIR, PAIR)
         copy_units(nc.scalar.copy, 1, PAIR, PAIR)
         project(0, 0, 0)
         project(0, 1, 0)
-        quantise_units(0, PAIR, PAIR)
+        transpose_wo_bank(1, 0)
         gate_unit(1, 0)
         gate_unit(1, 1)
-        transpose_wo_bank(1, 0)
         copy_wo_bank(nc.scalar.copy, 1, 0)
-        project(0, 2, 0)
         transpose_wo_bank(1, 1)
+        project(0, 2, 0)
         copy_wo_bank(nc.vector.tensor_copy, 1, 1)
-        project(0, 3, 0)
         gate_unit(1, 2)
         gate_unit(1, 3)
         quantise_wo_half(1)
-        multiply_group(1)
+        project(0, 3, 0)
+        multiply_by_gpsimd(1, 0)
         transpose_units(2, 0, PAIR)
         copy_units(nc.scalar.copy, 2, 0, PAIR)
         transpose_units(2, PAIR, PAIR)
@@ -318,17 +316,16 @@ def tile_gqaselfattention_pb_t_kernel(tc, attn, Wg, bg, Wo, bo, out):
         store(0, 0)
         project(0, 1, 1)
         store(0, 1)
-        multiply_rest(1)
         gate_unit(2, 0)
-        gate_unit(2, 1)
         project(0, 2, 1)
         store(0, 2)
+        gate_unit(2, 1)
+        quantise_units(1, 0, UNITS)
         project(0, 3, 1)
         store(0, 3)
-        quantise_units(1, 0, UNITS)
         gate_unit(2, 2)
         gate_unit(2, 3)
-        multiply_group(2)
+        multiply_by_gpsimd(2, VECTOR_TOKENS)
 
         for g in range(1, N_GROUPS):
             ahead = g + 2
@@ -342,7 +339,7 @@ def tile_gqaselfattention_pb_t_kernel(tc, attn, Wg, bg, Wo, bo, out):
                     elif half == C_HALVES - 1:
                         store(g, j)
                     if bank == 0 and g + 1 < N_GROUPS:
-                        multiply_rest(g + 1)
+                        multiply_by_vector(g + 1, VECTOR_TOKENS)
                     if ahead < N_GROUPS:
                         for first, when in ((0, 2), (PAIR, 3)):
                             if bank == when:
@@ -354,4 +351,4 @@ def tile_gqaselfattention_pb_t_kernel(tc, attn, Wg, bg, Wo, bo, out):
                     if bank == 5 and g + 1 < N_GROUPS:
                         quantise_units(g + 1, 0, UNITS)
                     if bank == 7 and ahead < N_GROUPS:
-                        multiply_group(ahead)
+                        multiply_by_gpsimd(ahead, VECTOR_TOKENS)

@@ -159,11 +159,15 @@ def tile_gqaselfattention_pb_t_kernel(tc, attn, Wg, bg, Wo, bo, out):
 
         def copy_units(copy, g, first, count):
             if first == 0:
-                at_sb = at_pool.tile([P, UNITS * UNIT, HEADS], BF16)
+                at_sb = at_pool.tile([P, UNITS * UNIT * HEADS], BF16)
                 attn_t[g] = at_sb
+            columns = slice(first * UNIT * HEADS, (first + count) * UNIT * HEADS)
             copy(
-                out=attn_t[g][:, first * UNIT : (first + count) * UNIT],
-                in_=attn_t_psum[g, first][:].rearrange("p t i q -> p (i q) t"),
+                out=attn_t[g][:, columns].bitcast(F32).rearrange("p (w t) -> p w t", t=HEADS),
+                in_=attn_t_psum[g, first][:]
+                .rearrange("p t i q -> p t (i q)")
+                .bitcast(F32)
+                .rearrange("p t w -> p w t"),
             )
 
         def gate_unit(g, j):
@@ -175,13 +179,13 @@ def tile_gqaselfattention_pb_t_kernel(tc, attn, Wg, bg, Wo, bo, out):
             nc.tensor.matmul(
                 out=z[:],
                 lhsT=wg_t[:],
-                rhs=attn_t[g][:, tokens].rearrange("p q t -> p (q t)"),
+                rhs=attn_t[g][:, j * UNIT * HEADS : (j + 1) * UNIT * HEADS],
                 start=True,
                 stop=True,
             )
             nc.scalar.activation(
-                out=gates[g][:, tokens].rearrange("p q t -> p (q t)"),
-                in_=z[:],
+                out=gates[g][:, tokens].rearrange("p (w e) t -> p w e t", e=2),
+                in_=z[:].rearrange("p (w t e) -> p w e t", t=HEADS, e=2),
                 func=SIGMOID,
                 bias=bg_col[:, 0:1],
             )
@@ -192,15 +196,21 @@ def tile_gqaselfattention_pb_t_kernel(tc, attn, Wg, bg, Wo, bo, out):
 
         def multiply(engine, g, tokens, attn_t_tokens):
             engine.tensor_tensor(
-                out=h_tiles[g][:, tokens],
-                in0=gates[g][:, tokens],
+                out=h_tiles[g][:, tokens].rearrange("p (w e) t -> p w e t", e=2),
+                in0=gates[g][:, tokens].rearrange("p (w e) t -> p w e t", e=2),
                 in1=attn_t_tokens,
                 op=MULT,
             )
 
         def multiply_sbuf(engine, g, first_token, last_token):
             tokens = slice(first_token, last_token)
-            multiply(engine, g, tokens, attn_t[g][:, tokens])
+            columns = slice(first_token * HEADS, last_token * HEADS)
+            multiply(
+                engine,
+                g,
+                tokens,
+                attn_t[g][:, columns].rearrange("p (w t e) -> p w e t", t=HEADS, e=2),
+            )
 
         def multiply_by_gpsimd(g, vector_tokens):
             new_h(g)
@@ -209,11 +219,12 @@ def tile_gqaselfattention_pb_t_kernel(tc, attn, Wg, bg, Wo, bo, out):
 
         def multiply_by_vector(g, vector_tokens):
             attn_t_pair = attn_t_psum[g, PAIR][:].rearrange("p t i q -> p (i q) t")
+            last_tokens = attn_t_pair[:, PAIR * UNIT - vector_tokens :]
             multiply(
                 nc.vector,
                 g,
                 slice(UNITS * UNIT - vector_tokens, UNITS * UNIT),
-                attn_t_pair[:, PAIR * UNIT - vector_tokens :],
+                last_tokens.rearrange("p (w e) t -> p w e t", e=2),
             )
 
         def quantise_units(g, first, count):
@@ -341,7 +352,7 @@ def tile_gqaselfattention_pb_t_kernel(tc, attn, Wg, bg, Wo, bo, out):
                     if bank == 0 and g + 1 < N_GROUPS:
                         multiply_by_vector(g + 1, VECTOR_TOKENS)
                     if ahead < N_GROUPS:
-                        for first, when in ((0, 2), (PAIR, 3)):
+                        for first, when in ((0, 1), (PAIR, 3)):
                             if bank == when:
                                 transpose_units(ahead, first, PAIR)
                                 copy_units(nc.scalar.copy, ahead, first, PAIR)

@@ -49,7 +49,7 @@ def tile_gqaselfattention_pb_t_kernel(tc, attn, Wg, bg, Wo, bo, out):
         attn_pool = ctx.enter_context(tc.tile_pool(name="attn", bufs=N_GROUPS))
         at_pool = ctx.enter_context(tc.tile_pool(name="attn_t", bufs=3))
         gate_pool = ctx.enter_context(tc.tile_pool(name="gate", bufs=3))
-        h_pool = ctx.enter_context(tc.tile_pool(name="h", bufs=1))
+        h_pool = ctx.enter_context(tc.tile_pool(name="h", bufs=2))
         mx_pool = ctx.enter_context(tc.tile_pool(name="h_mx", bufs=2))
         out_pool = ctx.enter_context(tc.tile_pool(name="out", bufs=6))
         psum = ctx.enter_context(tc.psum_pool(name="psum", bufs=1))

@@ -265,9 +265,12 @@ def tile_gqaselfattention_pb_t_kernel(tc, attn, Wg, bg, Wo, bo, out):
         def store(g, j, cols=slice(0, C_OUT)):
             nc.sync.dma_start(out=out_groups[g][:, j, cols], in_=out_tiles[g, j][:, cols])
 
-        for i in range(WARM):
-            junk = psum.tile([P, BANK_F32], F32, tag="acc", bufs=4)
-            nc.tensor.matmul(out=junk[:], lhsT=warm_rows[:, 0:P], rhs=warm_rows[:], start=True, stop=True)
+        def keep_warm(count):
+            for i in range(count):
+                junk = psum.tile([P, BANK_F32], F32, tag="acc", bufs=4)
+                nc.tensor.matmul(out=junk[:], lhsT=warm_rows[:, 0:P], rhs=warm_rows[:], start=True, stop=True)
+
+        keep_warm(WARM)
         wg_ps = transpose_small(wg_sb[:], "wg_ps")
         nc.vector.tensor_copy(out=wg_t[:], in_=wg_ps[:])
         transpose_units(0, 0, 1)
@@ -288,6 +291,7 @@ def tile_gqaselfattention_pb_t_kernel(tc, attn, Wg, bg, Wo, bo, out):
         copy_units(nc.scalar.copy, 0, 2, 1)
         transpose_units(0, 3, 1)
         copy_units(nc.scalar.copy, 0, 3, 1)
+        keep_warm(2)
         multiply_sbuf(nc.vector, 0, 0, UNIT)
         multiply_sbuf(nc.gpsimd, 0, UNIT, 2 * UNIT)
         transpose_wo_bank(0, 0)
@@ -305,33 +309,38 @@ def tile_gqaselfattention_pb_t_kernel(tc, attn, Wg, bg, Wo, bo, out):
         copy_units(nc.scalar.copy, 1, 0, PAIR)
         transpose_units(1, PAIR, PAIR)
         copy_units(nc.scalar.copy, 1, PAIR, PAIR)
+        keep_warm(1)
         project(0, 0, 0)
         project(0, 1, 0)
-        transpose_wo_bank(1, 0)
         gate_unit(1, 0)
         gate_unit(1, 1)
+        transpose_wo_bank(1, 0)
         copy_wo_bank(nc.scalar.copy, 1, 0)
         transpose_wo_bank(1, 1)
+        copy_wo_bank(nc.scalar.copy, 1, 1)
         project(0, 2, 0)
-        copy_wo_bank(nc.vector.tensor_copy, 1, 1)
+        project(0, 3, 0)
         gate_unit(1, 2)
         gate_unit(1, 3)
         quantise_wo_half(1)
-        project(0, 3, 0)
-        multiply_by_gpsimd(1, 0)
+        new_h(1)
+        multiply_sbuf(nc.gpsimd, 1, 0, UNIT)
+        multiply_sbuf(nc.gpsimd, 1, UNIT, 2 * UNIT)
+        multiply_sbuf(nc.gpsimd, 1, 2 * UNIT, 4 * UNIT - 128)
+        multiply_by_vector(1, 128)
         transpose_units(2, 0, PAIR)
         copy_units(nc.scalar.copy, 2, 0, PAIR)
-        transpose_units(2, PAIR, PAIR)
-        copy_units(nc.scalar.copy, 2, PAIR, PAIR)
         project(0, 0, 1)
         store(0, 0)
         project(0, 1, 1)
         store(0, 1)
         gate_unit(2, 0)
+        gate_unit(2, 1)
+        transpose_units(2, PAIR, PAIR)
+        copy_units(nc.scalar.copy, 2, PAIR, PAIR)
+        quantise_units(1, 0, UNITS)
         project(0, 2, 1)
         store(0, 2)
-        gate_unit(2, 1)
-        quantise_units(1, 0, UNITS)
         project(0, 3, 1)
         store(0, 3)
         gate_unit(2, 2)

@@ -51,7 +51,7 @@ def tile_gqaselfattention_pb_t_kernel(tc, attn, Wg, bg, Wo, bo, out):
         gate_pool = ctx.enter_context(tc.tile_pool(name="gate", bufs=3))
         h_pool = ctx.enter_context(tc.tile_pool(name="h", bufs=2))
         mx_pool = ctx.enter_context(tc.tile_pool(name="h_mx", bufs=2))
-        out_pool = ctx.enter_context(tc.tile_pool(name="out", bufs=6))
+        out_pool = ctx.enter_context(tc.tile_pool(name="out", bufs=24))
         psum = ctx.enter_context(tc.psum_pool(name="psum", bufs=1))
         ctx.enter_context(tc.manual_schedule())
 
@@ -81,10 +81,11 @@ def tile_gqaselfattention_pb_t_kernel(tc, attn, Wg, bg, Wo, bo, out):
                 out=attn_sb[g][:, first : first + count], in_=attn_groups[g][:, first : first + count]
             )
 
-        def load_wo_half(half):
+        def load_wo_bank(half, bank):
+            first = half * WO_BLOCKS + bank * BLOCKS_PER_BANK
             nc.sync.dma_start(
-                out=wo_sb[half][:],
-                in_=wo_rows[half * WO_BLOCKS * P : (half + 1) * WO_BLOCKS * P, :].rearrange(
+                out=wo_sb[half][:, bank * BLOCKS_PER_BANK : (bank + 1) * BLOCKS_PER_BANK],
+                in_=wo_rows[first * P : (first + BLOCKS_PER_BANK) * P, :].rearrange(
                     "(b p) f -> p b f", p=P
                 ),
             )
@@ -95,9 +96,11 @@ def tile_gqaselfattention_pb_t_kernel(tc, attn, Wg, bg, Wo, bo, out):
         nc.sync.dma_start(out=vec_rows[0:1, C_OUT : C_OUT + FEATURES], in_=bg.unsqueeze(0))
         nc.sync.dma_start(out=vec_rows[0:1, 0:C_OUT], in_=bo.unsqueeze(0))
         load_units(0, PAIR, PAIR)
-        load_wo_half(0)
+        load_wo_bank(0, 0)
+        load_wo_bank(0, 1)
         load_units(1, 0, UNITS)
-        load_wo_half(1)
+        load_wo_bank(1, 0)
+        load_wo_bank(1, 1)
         for g in range(2, N_GROUPS):
             load_units(g, 0, UNITS)
 
@@ -146,8 +149,8 @@ def tile_gqaselfattention_pb_t_kernel(tc, attn, Wg, bg, Wo, bo, out):
                 in_=wo_grouped[half][:],
             )
 
-        def transpose_units(g, first, count):
-            at_ps = psum.tile([P, HEADS, count, UNIT], BF16, tag="tr", bufs=2)
+        def transpose_units(g, first, count, tag="tr", bufs=2):
+            at_ps = psum.tile([P, HEADS, count, UNIT], BF16, tag=tag, bufs=bufs)
             attn_t_psum[g, first] = at_ps
             for i in range(count):
                 for t in range(HEADS):
@@ -265,6 +268,14 @@ def tile_gqaselfattention_pb_t_kernel(tc, attn, Wg, bg, Wo, bo, out):
         def store(g, j, cols=slice(0, C_OUT)):
             nc.sync.dma_start(out=out_groups[g][:, j, cols], in_=out_tiles[g, j][:, cols])
 
+        def project_bank(g, bank):
+            j, half = divmod(bank, C_HALVES)
+            project(g, j, half)
+            if g == N_GROUPS - 1 and j == UNITS - 1:
+                store(g, j, slice(half * BANK_F32, (half + 1) * BANK_F32))
+            elif half == C_HALVES - 1:
+                store(g, j)
+
         def keep_warm(count):
             for i in range(count):
                 junk = psum.tile([P, BANK_F32], F32, tag="acc", bufs=4)
@@ -300,17 +311,17 @@ def tile_gqaselfattention_pb_t_kernel(tc, attn, Wg, bg, Wo, bo, out):
         copy_wo_bank(nc.vector.tensor_copy, 0, 1)
         gate_unit(0, 2)
         gate_unit(0, 3)
-        quantise_wo_half(0)
         quantise_units(0, 0, PAIR)
+        quantise_wo_half(0)
         multiply_sbuf(nc.vector, 0, 2 * UNIT, 3 * UNIT)
         multiply_sbuf(nc.vector, 0, 3 * UNIT, 4 * UNIT)
-        quantise_units(0, PAIR, PAIR)
         transpose_units(1, 0, PAIR)
         copy_units(nc.scalar.copy, 1, 0, PAIR)
         transpose_units(1, PAIR, PAIR)
         copy_units(nc.scalar.copy, 1, PAIR, PAIR)
         keep_warm(1)
         project(0, 0, 0)
+        quantise_units(0, PAIR, PAIR)
         project(0, 1, 0)
         gate_unit(1, 0)
         gate_unit(1, 1)
@@ -343,32 +354,27 @@ def tile_gqaselfattention_pb_t_kernel(tc, attn, Wg, bg, Wo, bo, out):
         store(0, 2)
         project(0, 3, 1)
         store(0, 3)
+        project_bank(1, 0)
         gate_unit(2, 2)
+        project_bank(1, 1)
         gate_unit(2, 3)
         multiply_by_gpsimd(2, VECTOR_TOKENS)
 
         for g in range(1, N_GROUPS):
             ahead = g + 2
-            for j in range(UNITS):
-                for half in range(C_HALVES):
-                    bank = j * C_HALVES + half
-                    project(g, j, half)
-                    last = g == N_GROUPS - 1 and j == UNITS - 1
-                    if last:
-                        store(g, j, slice(half * BANK_F32, (half + 1) * BANK_F32))
-                    elif half == C_HALVES - 1:
-                        store(g, j)
-                    if bank == 0 and g + 1 < N_GROUPS:
-                        multiply_by_vector(g + 1, VECTOR_TOKENS)
-                    if ahead < N_GROUPS:
-                        for first, when in ((0, 1), (PAIR, 3)):
-                            if bank == when:
-                                transpose_units(ahead, first, PAIR)
-                                copy_units(nc.scalar.copy, ahead, first, PAIR)
-                        for unit, when in enumerate((4, 5, 6, 7)):
-                            if bank == when:
-                                gate_unit(ahead, unit)
-                    if bank == 5 and g + 1 < N_GROUPS:
-                        quantise_units(g + 1, 0, UNITS)
-                    if bank == 7 and ahead < N_GROUPS:
-                        multiply_by_gpsimd(ahead, VECTOR_TOKENS)
+            for bank in range(2 if g == 1 else 0, UNITS * C_HALVES):
+                project_bank(g, bank)
+                if bank == (2 if g == 1 else 0) and g + 1 < N_GROUPS:
+                    multiply_by_vector(g + 1, VECTOR_TOKENS)
+                if ahead < N_GROUPS:
+                    if bank == (4 if g == 1 else 3):
+                        for first in (0, PAIR):
+                            transpose_units(ahead, first, PAIR)
+                            copy_units(nc.scalar.copy, ahead, first, PAIR)
+                    if bank in (5, 7):
+                        gate_unit(ahead, bank - 5)
+                        gate_unit(ahead, bank - 4)
+                if bank == 5 and g + 1 < N_GROUPS:
+                    quantise_units(g + 1, 0, UNITS)
+                if bank == 7 and ahead < N_GROUPS:
+                    multiply_by_gpsimd(ahead, VECTOR_TOKENS)

@@ -51,7 +51,7 @@ def tile_gqaselfattention_pb_t_kernel(tc, attn, Wg, bg, Wo, bo, out):
         gate_pool = ctx.enter_context(tc.tile_pool(name="gate", bufs=3))
         h_pool = ctx.enter_context(tc.tile_pool(name="h", bufs=2))
         mx_pool = ctx.enter_context(tc.tile_pool(name="h_mx", bufs=2))
-        out_pool = ctx.enter_context(tc.tile_pool(name="out", bufs=24))
+        out_pool = ctx.enter_context(tc.tile_pool(name="out", bufs=12))
         psum = ctx.enter_context(tc.psum_pool(name="psum", bufs=1))
         ctx.enter_context(tc.manual_schedule())
 
@@ -246,10 +246,10 @@ def tile_gqaselfattention_pb_t_kernel(tc, attn, Wg, bg, Wo, bo, out):
         out_tiles = {}
 
         def project(g, j, half):
-            if (g, j) not in out_tiles:
-                out_sb = out_pool.tile([P, C_OUT], F32)
-                out_tiles[g, j] = out_sb
-            out_sb = out_tiles[g, j]
+            if j % PAIR == 0 and half == 0:
+                out_sb = out_pool.tile([P, PAIR, C_OUT], F32)
+                out_tiles[g, j // PAIR] = out_sb
+            out_sb = out_tiles[g, j // PAIR][:, j % PAIR]
             words, scales = h_mx[g]
             tokens = slice(j * UNIT, (j + 1) * UNIT)
             cols = slice(half * BANK_F32, (half + 1) * BANK_F32)
@@ -266,15 +266,27 @@ def tile_gqaselfattention_pb_t_kernel(tc, attn, Wg, bg, Wo, bo, out):
             nc.vector.tensor_tensor(out=out_sb[:, cols], in0=acc[:], in1=bo_all[:, cols], op=ADD)
 
         def store(g, j, cols=slice(0, C_OUT)):
-            nc.sync.dma_start(out=out_groups[g][:, j, cols], in_=out_tiles[g, j][:, cols])
+            nc.sync.dma_start(out=out_groups[g][:, j, cols], in_=out_tiles[g, j // PAIR][:, j % PAIR, cols])
+
+        def store_half(g, j, half):
+            store(g, j, slice(half * BANK_F32, (half + 1) * BANK_F32))
+
+        def store_pair(g, first):
+            nc.sync.dma_start(
+                out=out_groups[g][:, first : first + PAIR, :], in_=out_tiles[g, first // PAIR][:]
+            )
 
         def project_bank(g, bank):
             j, half = divmod(bank, C_HALVES)
             project(g, j, half)
-            if g == N_GROUPS - 1 and j == UNITS - 1:
-                store(g, j, slice(half * BANK_F32, (half + 1) * BANK_F32))
+            unit = g * UNITS + j
+            if unit == N_GROUPS * UNITS - 1:
+                store_half(g, j, half)
             elif half == C_HALVES - 1:
-                store(g, j)
+                if unit >= (N_GROUPS - 1) * UNITS - PAIR:
+                    store(g, j)
+                elif j % PAIR == PAIR - 1:
+                    store_pair(g, j - 1)
 
         def keep_warm(count):
             for i in range(count):
@@ -321,8 +333,10 @@ def tile_gqaselfattention_pb_t_kernel(tc, attn, Wg, bg, Wo, bo, out):
         copy_units(nc.scalar.copy, 1, PAIR, PAIR)
         keep_warm(1)
         project(0, 0, 0)
+        store_half(0, 0, 0)
         quantise_units(0, PAIR, PAIR)
         project(0, 1, 0)
+        store_half(0, 1, 0)
         gate_unit(1, 0)
         gate_unit(1, 1)
         transpose_wo_bank(1, 0)
@@ -330,7 +344,9 @@ def tile_gqaselfattention_pb_t_kernel(tc, attn, Wg, bg, Wo, bo, out):
         transpose_wo_bank(1, 1)
         copy_wo_bank(nc.scalar.copy, 1, 1)
         project(0, 2, 0)
+        store_half(0, 2, 0)
         project(0, 3, 0)
+        store_half(0, 3, 0)
         gate_unit(1, 2)
         gate_unit(1, 3)
         quantise_wo_half(1)
@@ -342,18 +358,18 @@ def tile_gqaselfattention_pb_t_kernel(tc, attn, Wg, bg, Wo, bo, out):
         transpose_units(2, 0, PAIR)
         copy_units(nc.scalar.copy, 2, 0, PAIR)
         project(0, 0, 1)
-        store(0, 0)
+        store_half(0, 0, 1)
         project(0, 1, 1)
-        store(0, 1)
+        store_half(0, 1, 1)
         gate_unit(2, 0)
         gate_unit(2, 1)
         transpose_units(2, PAIR, PAIR)
         copy_units(nc.scalar.copy, 2, PAIR, PAIR)
         quantise_units(1, 0, UNITS)
         project(0, 2, 1)
-        store(0, 2)
+        store_half(0, 2, 1)
         project(0, 3, 1)
-        store(0, 3)
+        store_half(0, 3, 1)
         project_bank(1, 0)
         gate_unit(2, 2)
         project_bank(1, 1)

@@ -29,8 +29,11 @@ N_GROUPS = TOKENS // (UNIT * UNITS)
 VECTOR_TOKENS = 64
 WARM = 3
 
-WO_BLOCKS = BANK_F32 * HEADS // P
-BLOCKS_PER_BANK = BANK_BF16 // P
+RUNS = 2
+RUN_HEADS = HEADS // RUNS
+HEAD_OF_SLOT = [run * RUN_HEADS + i for i in range(RUN_HEADS) for run in range(RUNS)]
+WO_BLOCKS = BANK_F32 * RUNS // P
+BLOCKS_PER_BANK = BANK_BF16 // (P * RUN_HEADS)
 
 FLOPS = 2 * TOKENS * HEADS * FEATURES * FEATURES + 2 * TOKENS * K * C_OUT
 
@@ -38,15 +41,15 @@ FLOPS = 2 * TOKENS * HEADS * FEATURES * FEATURES + 2 * TOKENS * K * C_OUT
 def tile_gqaselfattention_pb_t_kernel(tc, attn, Wg, bg, Wo, bo, out):
     nc = tc.nc
 
-    attn_groups = attn.rearrange("b s h d -> (b s) (h d)").rearrange(
-        "(g q j) k -> g q j k", q=P, j=UNITS
+    attn_twos = attn.rearrange("b s h d -> (b s) (h d)").rearrange(
+        "(g q j) k -> g q j k", q=P, j=2 * UNITS
     )
-    out_groups = out.rearrange("b s c -> (b s) c").rearrange("(g q j) c -> g q j c", q=P, j=UNITS)
-    wo_rows = Wo.rearrange("c (t f) -> (c t) f", f=FEATURES)
+    out_twos = out.rearrange("b s c -> (b s) c").rearrange("(g q j) c -> g q j c", q=P, j=2 * UNITS)
+    wo_runs = Wo.rearrange("c (r k) -> (c r) k", r=RUNS)
 
     with ExitStack() as ctx:
         const = ctx.enter_context(tc.tile_pool(name="const", bufs=1))
-        attn_pool = ctx.enter_context(tc.tile_pool(name="attn", bufs=N_GROUPS))
+        attn_pool = ctx.enter_context(tc.tile_pool(name="attn", bufs=N_GROUPS // 2))
         at_pool = ctx.enter_context(tc.tile_pool(name="attn_t", bufs=3))
         gate_pool = ctx.enter_context(tc.tile_pool(name="gate", bufs=3))
         h_pool = ctx.enter_context(tc.tile_pool(name="h", bufs=2))
@@ -68,25 +71,27 @@ def tile_gqaselfattention_pb_t_kernel(tc, attn, Wg, bg, Wo, bo, out):
 
         wg_sb = const.tile([P, FEATURES], BF16)
         attn_sb = []
-        for g in range(N_GROUPS):
-            attn_g = attn_pool.tile([P, UNITS, K], BF16)
+        for g in range(N_GROUPS // 2):
+            attn_g = attn_pool.tile([P, 2 * UNITS, K], BF16)
             attn_sb.append(attn_g)
         wo_sb = []
         for half in range(C_HALVES):
-            wo_half = const.tile([P, WO_BLOCKS, FEATURES], BF16, name="wo_half%d" % half)
+            wo_half = const.tile([P, WO_BLOCKS, RUN_HEADS * FEATURES], BF16, name="wo_half%d" % half)
             wo_sb.append(wo_half)
 
         def load_units(g, first, count):
+            first += g % 2 * UNITS
             nc.sync.dma_start(
-                out=attn_sb[g][:, first : first + count], in_=attn_groups[g][:, first : first + count]
+                out=attn_sb[g // 2][:, first : first + count],
+                in_=attn_twos[g // 2][:, first : first + count],
             )
 
         def load_wo_bank(half, bank):
             first = half * WO_BLOCKS + bank * BLOCKS_PER_BANK
             nc.sync.dma_start(
                 out=wo_sb[half][:, bank * BLOCKS_PER_BANK : (bank + 1) * BLOCKS_PER_BANK],
-                in_=wo_rows[first * P : (first + BLOCKS_PER_BANK) * P, :].rearrange(
-                    "(b p) f -> p b f", p=P
+                in_=wo_runs[first * P : (first + BLOCKS_PER_BANK) * P, :].rearrange(
+                    "(b p) k -> p b k", p=P
                 ),
             )
 
@@ -101,8 +106,8 @@ def tile_gqaselfattention_pb_t_kernel(tc, attn, Wg, bg, Wo, bo, out):
         load_units(1, 0, UNITS)
         load_wo_bank(1, 0)
         load_wo_bank(1, 1)
-        for g in range(2, N_GROUPS):
-            load_units(g, 0, UNITS)
+        for g in range(2, N_GROUPS, 2):
+            load_units(g, 0, 2 * UNITS)
 
         wg_t = const.tile([P, FEATURES], BF16)
         bg_col = const.tile([P, 1], F32)
@@ -126,19 +131,23 @@ def tile_gqaselfattention_pb_t_kernel(tc, attn, Wg, bg, Wo, bo, out):
             return ps
 
         def transpose_wo_bank(half, bank):
-            wo_t = psum.tile([P, BLOCKS_PER_BANK, P], BF16, tag="acc", bufs=4)
-            for i in range(BLOCKS_PER_BANK):
-                nc.tensor.transpose(
-                    out=wo_t[:, i, :],
-                    in_=wo_sb[half][:, bank * BLOCKS_PER_BANK + i, :],
-                    identity=ident[:],
-                )
+            wo_t = psum.tile([P, BLOCKS_PER_BANK, RUN_HEADS, P], BF16, tag="acc", bufs=4)
+            for b in range(BLOCKS_PER_BANK):
+                for i in range(RUN_HEADS):
+                    nc.tensor.transpose(
+                        out=wo_t[:, b, i, :],
+                        in_=wo_sb[half][:, bank * BLOCKS_PER_BANK + b, i * FEATURES : (i + 1) * FEATURES],
+                        identity=ident[:],
+                    )
             wo_t_psum[half, bank] = wo_t
 
         def copy_wo_bank(copy, half, bank):
+            grouped = wo_grouped[half][:, bank * BANK_BF16 : (bank + 1) * BANK_BF16]
             copy(
-                out=wo_grouped[half][:, bank * BANK_BF16 : (bank + 1) * BANK_BF16],
-                in_=wo_t_psum[half, bank][:].rearrange("p i c -> p (i c)"),
+                out=grouped.bitcast(F32).rearrange(
+                    "p (b c i) -> p b c i", b=BLOCKS_PER_BANK, i=RUN_HEADS
+                ),
+                in_=wo_t_psum[half, bank][:].bitcast(F32).rearrange("p b i c -> p b c i"),
             )
 
         def quantise_wo_half(half):
@@ -153,10 +162,11 @@ def tile_gqaselfattention_pb_t_kernel(tc, attn, Wg, bg, Wo, bo, out):
             at_ps = psum.tile([P, HEADS, count, UNIT], BF16, tag=tag, bufs=bufs)
             attn_t_psum[g, first] = at_ps
             for i in range(count):
-                for t in range(HEADS):
+                for s in range(HEADS):
+                    t = HEAD_OF_SLOT[s]
                     nc.tensor.transpose(
-                        out=at_ps[:, t, i, :],
-                        in_=attn_sb[g][:, first + i, t * FEATURES : (t + 1) * FEATURES],
+                        out=at_ps[:, s, i, :],
+                        in_=attn_sb[g // 2][:, g % 2 * UNITS + first + i, t * FEATURES : (t + 1) * FEATURES],
                         identity=ident[:],
                     )
 
@@ -266,14 +276,18 @@ def tile_gqaselfattention_pb_t_kernel(tc, attn, Wg, bg, Wo, bo, out):
             nc.vector.tensor_tensor(out=out_sb[:, cols], in0=acc[:], in1=bo_all[:, cols], op=ADD)
 
         def store(g, j, cols=slice(0, C_OUT)):
-            nc.sync.dma_start(out=out_groups[g][:, j, cols], in_=out_tiles[g, j // PAIR][:, j % PAIR, cols])
+            nc.sync.dma_start(
+                out=out_twos[g // 2][:, g % 2 * UNITS + j, cols],
+                in_=out_tiles[g, j // PAIR][:, j % PAIR, cols],
+            )
 
         def store_half(g, j, half):
             store(g, j, slice(half * BANK_F32, (half + 1) * BANK_F32))
 
         def store_pair(g, first):
             nc.sync.dma_start(
-                out=out_groups[g][:, first : first + PAIR, :], in_=out_tiles[g, first // PAIR][:]
+                out=out_twos[g // 2][:, g % 2 * UNITS + first : g % 2 * UNITS + first + PAIR, :],
+                in_=out_tiles[g, first // PAIR][:],
             )
 
         def project_bank(g, bank):

@@ -328,13 +328,13 @@ def tile_gqaselfattention_pb_t_kernel(tc, attn, Wg, bg, Wo, bo, out):
         copy_units(nc.scalar.copy, 0, 2, 1)
         transpose_units(0, 3, 1)
         copy_units(nc.scalar.copy, 0, 3, 1)
-        keep_warm(2)
         multiply_sbuf(nc.vector, 0, 0, UNIT)
         multiply_sbuf(nc.gpsimd, 0, UNIT, 2 * UNIT)
         transpose_wo_bank(0, 0)
         copy_wo_bank(nc.vector.tensor_copy, 0, 0)
         transpose_wo_bank(0, 1)
         copy_wo_bank(nc.vector.tensor_copy, 0, 1)
+        keep_warm(2)
         gate_unit(0, 2)
         gate_unit(0, 3)
         quantise_units(0, 0, PAIR)
@@ -345,34 +345,33 @@ def tile_gqaselfattention_pb_t_kernel(tc, attn, Wg, bg, Wo, bo, out):
         copy_units(nc.scalar.copy, 1, 0, PAIR)
         transpose_units(1, PAIR, PAIR)
         copy_units(nc.scalar.copy, 1, PAIR, PAIR)
-        keep_warm(1)
+        transpose_wo_bank(1, 0)
+        copy_wo_bank(nc.scalar.copy, 1, 0)
         project(0, 0, 0)
         store_half(0, 0, 0)
         quantise_units(0, PAIR, PAIR)
         project(0, 1, 0)
         store_half(0, 1, 0)
-        gate_unit(1, 0)
-        gate_unit(1, 1)
-        transpose_wo_bank(1, 0)
-        copy_wo_bank(nc.scalar.copy, 1, 0)
         transpose_wo_bank(1, 1)
         copy_wo_bank(nc.scalar.copy, 1, 1)
+        quantise_wo_half(1)
+        gate_unit(1, 0)
+        gate_unit(1, 1)
         project(0, 2, 0)
         store_half(0, 2, 0)
         project(0, 3, 0)
         store_half(0, 3, 0)
         gate_unit(1, 2)
+        project(0, 0, 1)
+        store_half(0, 0, 1)
         gate_unit(1, 3)
-        quantise_wo_half(1)
         new_h(1)
         multiply_sbuf(nc.gpsimd, 1, 0, UNIT)
         multiply_sbuf(nc.gpsimd, 1, UNIT, 2 * UNIT)
-        multiply_sbuf(nc.gpsimd, 1, 2 * UNIT, 4 * UNIT - 128)
-        multiply_by_vector(1, 128)
+        multiply_sbuf(nc.gpsimd, 1, 2 * UNIT, 320)
+        multiply_by_vector(1, 192)
         transpose_units(2, 0, PAIR)
         copy_units(nc.scalar.copy, 2, 0, PAIR)
-        project(0, 0, 1)
-        store_half(0, 0, 1)
         project(0, 1, 1)
         store_half(0, 1, 1)
         gate_unit(2, 0)
@@ -397,13 +396,12 @@ def tile_gqaselfattention_pb_t_kernel(tc, attn, Wg, bg, Wo, bo, out):
                 if bank == (2 if g == 1 else 0) and g + 1 < N_GROUPS:
                     multiply_by_vector(g + 1, VECTOR_TOKENS)
                 if ahead < N_GROUPS:
-                    if bank == (4 if g == 1 else 3):
-                        for first in (0, PAIR):
+                    for first, when in ((0, 2 if g == 1 else 1), (PAIR, 4 if g == 1 else 3)):
+                        if bank == when:
                             transpose_units(ahead, first, PAIR)
                             copy_units(nc.scalar.copy, ahead, first, PAIR)
-                    if bank in (5, 7):
-                        gate_unit(ahead, bank - 5)
-                        gate_unit(ahead, bank - 4)
+                    if bank >= UNITS:
+                        gate_unit(ahead, bank - UNITS)
                 if bank == 5 and g + 1 < N_GROUPS:
                     quantise_units(g + 1, 0, UNITS)
                 if bank == 7 and ahead < N_GROUPS:

from contextlib import ExitStack

import concourse.mybir as mybir
from concourse.masks import make_identity

BF16 = mybir.dt.bfloat16
F32 = mybir.dt.float32
U32 = mybir.dt.uint32
U8 = mybir.dt.uint8
FP8X4 = mybir.dt.float8_e4m3fn_x4
SIGMOID = mybir.ActivationFunctionType.Sigmoid
MULT = mybir.AluOpType.mult
ADD = mybir.AluOpType.add

P = 128
TOKENS = 4 * 1024
HEADS = 4
FEATURES = 128
K = HEADS * FEATURES
C_OUT = 1024
BANK_F32 = 512
BANK_BF16 = 2 * BANK_F32
C_HALVES = C_OUT // BANK_F32

UNIT = 128
UNITS = 4
PAIR = 2
N_GROUPS = TOKENS // (UNIT * UNITS)
VECTOR_TOKENS = 64
WARM = 3

RUNS = 2
RUN_HEADS = HEADS // RUNS
HEAD_OF_SLOT = [run * RUN_HEADS + i for i in range(RUN_HEADS) for run in range(RUNS)]
WO_BLOCKS = BANK_F32 * RUNS // P
BLOCKS_PER_BANK = BANK_BF16 // (P * RUN_HEADS)

FLOPS = 2 * TOKENS * HEADS * FEATURES * FEATURES + 2 * TOKENS * K * C_OUT


def tile_gqaselfattention_pb_t_kernel(tc, attn, Wg, bg, Wo, bo, out):
    nc = tc.nc

    attn_twos = attn.rearrange("b s h d -> (b s) (h d)").rearrange(
        "(g q j) k -> g q j k", q=P, j=2 * UNITS
    )
    out_twos = out.rearrange("b s c -> (b s) c").rearrange("(g q j) c -> g q j c", q=P, j=2 * UNITS)
    wo_runs = Wo.rearrange("c (r k) -> (c r) k", r=RUNS)

    with ExitStack() as ctx:
        const = ctx.enter_context(tc.tile_pool(name="const", bufs=1))
        attn_pool = ctx.enter_context(tc.tile_pool(name="attn", bufs=N_GROUPS // 2))
        at_pool = ctx.enter_context(tc.tile_pool(name="attn_t", bufs=3))
        gate_pool = ctx.enter_context(tc.tile_pool(name="gate", bufs=3))
        h_pool = ctx.enter_context(tc.tile_pool(name="h", bufs=2))
        mx_pool = ctx.enter_context(tc.tile_pool(name="h_mx", bufs=2))
        out_pool = ctx.enter_context(tc.tile_pool(name="out", bufs=12))
        psum = ctx.enter_context(tc.psum_pool(name="psum", bufs=1))
        ctx.enter_context(tc.manual_schedule())

        vec_rows = const.tile([P, C_OUT + FEATURES], BF16)
        nc.vector.memset(vec_rows[:].bitcast(F32), 0.0)
        warm_rows = const.tile([P, BANK_F32], BF16)
        nc.vector.memset(warm_rows[:].bitcast(F32), 0.0)
        ident = const.tile([P, P], BF16)
        make_identity(nc, ident[:])
        ones = const.tile([P, P], BF16)
        nc.vector.memset(ones[:], 1.0)
        warm = const.tile([P, 1], F32)
        nc.scalar.activation(out=warm[:], in_=ones[:, 0:1], func=SIGMOID)

        wg_sb = const.tile([P, FEATURES], BF16)
        attn_sb = []
        for g in range(N_GROUPS // 2):
            attn_g = attn_pool.tile([P, 2 * UNITS, K], BF16)
            attn_sb.append(attn_g)
        wo_sb = []
        for half in range(C_HALVES):
            wo_half = const.tile([P, WO_BLOCKS, RUN_HEADS * FEATURES], BF16, name="wo_half%d" % half)
            wo_sb.append(wo_half)

        def load_units(g, first, count):
            first += g % 2 * UNITS
            nc.sync.dma_start(
                out=attn_sb[g // 2][:, first : first + count],
                in_=attn_twos[g // 2][:, first : first + count],
            )

        def load_wo_bank(half, bank):
            first = half * WO_BLOCKS + bank * BLOCKS_PER_BANK
            nc.sync.dma_start(
                out=wo_sb[half][:, bank * BLOCKS_PER_BANK : (bank + 1) * BLOCKS_PER_BANK],
                in_=wo_runs[first * P : (first + BLOCKS_PER_BANK) * P, :].rearrange(
                    "(b p) k -> p b k", p=P
                ),
            )

        nc.sync.dma_start(out=wg_sb[:], in_=Wg)
        load_units(0, 0, 1)
        load_units(0, 1, 1)
        nc.sync.dma_start(out=vec_rows[0:1, C_OUT : C_OUT + FEATURES], in_=bg.unsqueeze(0))
        nc.sync.dma_start(out=vec_rows[0:1, 0:C_OUT], in_=bo.unsqueeze(0))
        load_units(0, PAIR, PAIR)
        load_wo_bank(0, 0)
        load_wo_bank(0, 1)
        load_units(1, 0, UNITS)
        load_wo_bank(1, 0)
        load_wo_bank(1, 1)
        for g in range(2, N_GROUPS, 2):
            load_units(g, 0, 2 * UNITS)

        wg_t = const.tile([P, FEATURES], BF16)
        bg_col = const.tile([P, 1], F32)
        bo_all = const.tile([P, C_OUT], F32)
        wo_words = const.tile([P, C_OUT], U32, align_bytes=64)
        wo_scales = const.tile([P, C_OUT], U8, align_bytes=64)
        wo_grouped = []
        for half in range(C_HALVES):
            grouped = const.tile([P, BANK_F32 * HEADS], BF16, align_bytes=64, name="wo_grouped%d" % half)
            wo_grouped.append(grouped)
        wo_t_psum = {}
        attn_t_psum = {}
        attn_t = {}
        gates = {}
        h_tiles = {}
        h_mx = {}

        def transpose_small(columns_of, name):
            ps = psum.tile([P, P], BF16, tag="z", bufs=2, name=name)
            nc.tensor.transpose(out=ps[:], in_=columns_of, identity=ident[:])
            return ps

        def transpose_wo_bank(half, bank):
            wo_t = psum.tile([P, BLOCKS_PER_BANK, RUN_HEADS, P], BF16, tag="acc", bufs=4)
            for b in range(BLOCKS_PER_BANK):
                for i in range(RUN_HEADS):
                    nc.tensor.transpose(
                        out=wo_t[:, b, i, :],
                        in_=wo_sb[half][:, bank * BLOCKS_PER_BANK + b, i * FEATURES : (i + 1) * FEATURES],
                        identity=ident[:],
                    )
            wo_t_psum[half, bank] = wo_t

        def copy_wo_bank(copy, half, bank):
            grouped = wo_grouped[half][:, bank * BANK_BF16 : (bank + 1) * BANK_BF16]
            copy(
                out=grouped.bitcast(F32).rearrange(
                    "p (b c i) -> p b c i", b=BLOCKS_PER_BANK, i=RUN_HEADS
                ),
                in_=wo_t_psum[half, bank][:].bitcast(F32).rearrange("p b i c -> p b c i"),
            )

        def quantise_wo_half(half):
            cols = slice(half * BANK_F32, (half + 1) * BANK_F32)
            nc.vector.quantize_mx(
                out=wo_words[:, cols].bitcast(FP8X4),
                scales=wo_scales[:, cols],
                in_=wo_grouped[half][:],
            )

        def transpose_units(g, first, count, tag="tr", bufs=2):
            at_ps = psum.tile([P, HEADS, count, UNIT], BF16, tag=tag, bufs=bufs)
            attn_t_psum[g, first] = at_ps
            for i in range(count):
                for s in range(HEADS):
                    t = HEAD_OF_SLOT[s]
                    nc.tensor.transpose(
                        out=at_ps[:, s, i, :],
                        in_=attn_sb[g // 2][:, g % 2 * UNITS + first + i, t * FEATURES : (t + 1) * FEATURES],
                        identity=ident[:],
                    )

        def copy_units(copy, g, first, count):
            if first == 0:
                at_sb = at_pool.tile([P, UNITS * UNIT * HEADS], BF16)
                attn_t[g] = at_sb
            columns = slice(first * UNIT * HEADS, (first + count) * UNIT * HEADS)
            copy(
                out=attn_t[g][:, columns].bitcast(F32).rearrange("p (w t) -> p w t", t=HEADS),
                in_=attn_t_psum[g, first][:]
                .rearrange("p t i q -> p t (i q)")
                .bitcast(F32)
                .rearrange("p t w -> p w t"),
            )

        def gate_unit(g, j):
            if j == 0:
                gate_g = gate_pool.tile([P, UNITS * UNIT, HEADS], F32)
                gates[g] = gate_g
            tokens = slice(j * UNIT, (j + 1) * UNIT)
            z = psum.tile([P, UNIT * HEADS], F32, tag="z", bufs=2)
            nc.tensor.matmul(
                out=z[:],
                lhsT=wg_t[:],
                rhs=attn_t[g][:, j * UNIT * HEADS : (j + 1) * UNIT * HEADS],
                start=True,
                stop=True,
            )
            nc.scalar.activation(
                out=gates[g][:, tokens].rearrange("p (w e) t -> p w e t", e=2),
                in_=z[:].rearrange("p (w t e) -> p w e t", t=HEADS, e=2),
                func=SIGMOID,
                bias=bg_col[:, 0:1],
            )

        def new_h(g):
            h = h_pool.tile([P, UNITS * UNIT, HEADS], BF16, align_bytes=64)
            h_tiles[g] = h

        def multiply(engine, g, tokens, attn_t_tokens):
            engine.tensor_tensor(
                out=h_tiles[g][:, tokens].rearrange("p (w e) t -> p w e t", e=2),
                in0=gates[g][:, tokens].rearrange("p (w e) t -> p w e t", e=2),
                in1=attn_t_tokens,
                op=MULT,
            )

        def multiply_sbuf(engine, g, first_token, last_token):
            tokens = slice(first_token, last_token)
            columns = slice(first_token * HEADS, last_token * HEADS)
            multiply(
                engine,
                g,
                tokens,
                attn_t[g][:, columns].rearrange("p (w t e) -> p w e t", t=HEADS, e=2),
            )

        def multiply_by_gpsimd(g, vector_tokens):
            new_h(g)
            multiply_sbuf(nc.gpsimd, g, 0, PAIR * UNIT)
            multiply_sbuf(nc.gpsimd, g, PAIR * UNIT, UNITS * UNIT - vector_tokens)

        def multiply_by_vector(g, vector_tokens):
            attn_t_pair = attn_t_psum[g, PAIR][:].rearrange("p t i q -> p (i q) t")
            last_tokens = attn_t_pair[:, PAIR * UNIT - vector_tokens :]
            multiply(
                nc.vector,
                g,
                slice(UNITS * UNIT - vector_tokens, UNITS * UNIT),
                last_tokens.rearrange("p (w e) t -> p w e t", e=2),
            )

        def quantise_units(g, first, count):
            if first == 0:
                words = mx_pool.tile([P, UNITS * UNIT], U32, align_bytes=64)
                scales = mx_pool.tile([P, UNITS * UNIT], U8, align_bytes=64)
                h_mx[g] = (words, scales)
            words, scales = h_mx[g]
            tokens = slice(first * UNIT, (first + count) * UNIT)
            nc.vector.quantize_mx(
                out=words[:, tokens].bitcast(FP8X4),
                scales=scales[:, tokens],
                in_=h_tiles[g][:, tokens].rearrange("p q t -> p (q t)"),
            )

        out_tiles = {}

        def project(g, j, half):
            if j % PAIR == 0 and half == 0:
                out_sb = out_pool.tile([P, PAIR, C_OUT], F32)
                out_tiles[g, j // PAIR] = out_sb
            out_sb = out_tiles[g, j // PAIR][:, j % PAIR]
            words, scales = h_mx[g]
            tokens = slice(j * UNIT, (j + 1) * UNIT)
            cols = slice(half * BANK_F32, (half + 1) * BANK_F32)
            acc = psum.tile([P, BANK_F32], F32, tag="acc", bufs=4)
            nc.tensor.matmul_mx(
                out=acc[:],
                lhsT=words[:, tokens].bitcast(FP8X4),
                lhsT_scale=scales[:, tokens],
                rhs=wo_words[:, cols].bitcast(FP8X4),
                rhs_scale=wo_scales[:, cols],
                start=True,
                stop=True,
            )
            nc.vector.tensor_tensor(out=out_sb[:, cols], in0=acc[:], in1=bo_all[:, cols], op=ADD)

        def store(g, j, cols=slice(0, C_OUT)):
            nc.sync.dma_start(
                out=out_twos[g // 2][:, g % 2 * UNITS + j, cols],
                in_=out_tiles[g, j // PAIR][:, j % PAIR, cols],
            )

        def store_half(g, j, half):
            store(g, j, slice(half * BANK_F32, (half + 1) * BANK_F32))

        def store_pair(g, first):
            nc.sync.dma_start(
                out=out_twos[g // 2][:, g % 2 * UNITS + first : g % 2 * UNITS + first + PAIR, :],
                in_=out_tiles[g, first // PAIR][:],
            )

        def project_bank(g, bank):
            j, half = divmod(bank, C_HALVES)
            project(g, j, half)
            unit = g * UNITS + j
            if unit == N_GROUPS * UNITS - 1:
                store_half(g, j, half)
            elif half == C_HALVES - 1:
                if unit >= (N_GROUPS - 1) * UNITS - PAIR:
                    store(g, j)
                elif j % PAIR == PAIR - 1:
                    store_pair(g, j - 1)

        def keep_warm(count):
            for i in range(count):
                junk = psum.tile([P, BANK_F32], F32, tag="acc", bufs=4)
                nc.tensor.matmul(out=junk[:], lhsT=warm_rows[:, 0:P], rhs=warm_rows[:], start=True, stop=True)

        keep_warm(WARM)
        wg_ps = transpose_small(wg_sb[:], "wg_ps")
        nc.vector.tensor_copy(out=wg_t[:], in_=wg_ps[:])
        transpose_units(0, 0, 1)
        copy_units(nc.scalar.copy, 0, 0, 1)
        transpose_units(0, 1, 1)
        copy_units(nc.vector.tensor_copy, 0, 1, 1)
        bg_ps = transpose_small(vec_rows[:, C_OUT : C_OUT + FEATURES], "bg_ps")
        nc.vector.tensor_copy(out=bg_col[:], in_=bg_ps[:, 0:1])
        for half, copy in enumerate((nc.scalar.copy, nc.vector.tensor_copy)):
            cols = slice(half * BANK_F32, (half + 1) * BANK_F32)
            bo_ps = psum.tile([P, BANK_F32], F32, tag="acc", bufs=4)
            nc.tensor.matmul(out=bo_ps[:], lhsT=ones[:], rhs=vec_rows[:, cols], start=True, stop=True)
            copy(out=bo_all[:, cols], in_=bo_ps[:])
        new_h(0)
        gate_unit(0, 0)
        gate_unit(0, 1)
        transpose_units(0, 2, 1)
        copy_units(nc.scalar.copy, 0, 2, 1)
        transpose_units(0, 3, 1)
        copy_units(nc.scalar.copy, 0, 3, 1)
        multiply_sbuf(nc.vector, 0, 0, UNIT)
        multiply_sbuf(nc.gpsimd, 0, UNIT, 2 * UNIT)
        transpose_wo_bank(0, 0)
        copy_wo_bank(nc.vector.tensor_copy, 0, 0)
        transpose_wo_bank(0, 1)
        copy_wo_bank(nc.vector.tensor_copy, 0, 1)
        keep_warm(2)
        gate_unit(0, 2)
        gate_unit(0, 3)
        quantise_units(0, 0, PAIR)
        quantise_wo_half(0)
        multiply_sbuf(nc.vector, 0, 2 * UNIT, 3 * UNIT)
        multiply_sbuf(nc.vector, 0, 3 * UNIT, 4 * UNIT)
        transpose_units(1, 0, PAIR)
        copy_units(nc.scalar.copy, 1, 0, PAIR)
        transpose_units(1, PAIR, PAIR)
        copy_units(nc.scalar.copy, 1, PAIR, PAIR)
        transpose_wo_bank(1, 0)
        copy_wo_bank(nc.scalar.copy, 1, 0)
        project(0, 0, 0)
        store_half(0, 0, 0)
        quantise_units(0, PAIR, PAIR)
        project(0, 1, 0)
        store_half(0, 1, 0)
        transpose_wo_bank(1, 1)
        copy_wo_bank(nc.scalar.copy, 1, 1)
        quantise_wo_half(1)
        gate_unit(1, 0)
        gate_unit(1, 1)
        project(0, 2, 0)
        store_half(0, 2, 0)
        project(0, 3, 0)
        store_half(0, 3, 0)
        gate_unit(1, 2)
        project(0, 0, 1)
        store_half(0, 0, 1)
        gate_unit(1, 3)
        new_h(1)
        multiply_sbuf(nc.gpsimd, 1, 0, UNIT)
        multiply_sbuf(nc.gpsimd, 1, UNIT, 2 * UNIT)
        multiply_sbuf(nc.gpsimd, 1, 2 * UNIT, 320)
        multiply_by_vector(1, 192)
        transpose_units(2, 0, PAIR)
        copy_units(nc.scalar.copy, 2, 0, PAIR)
        project(0, 1, 1)
        store_half(0, 1, 1)
        gate_unit(2, 0)
        gate_unit(2, 1)
        transpose_units(2, PAIR, PAIR)
        copy_units(nc.scalar.copy, 2, PAIR, PAIR)
        quantise_units(1, 0, UNITS)
        project(0, 2, 1)
        store_half(0, 2, 1)
        project(0, 3, 1)
        store_half(0, 3, 1)
        project_bank(1, 0)
        gate_unit(2, 2)
        project_bank(1, 1)
        gate_unit(2, 3)
        multiply_by_gpsimd(2, VECTOR_TOKENS)

        for g in range(1, N_GROUPS):
            ahead = g + 2
            for bank in range(2 if g == 1 else 0, UNITS * C_HALVES):
                project_bank(g, bank)
                if bank == (2 if g == 1 else 0) and g + 1 < N_GROUPS:
                    multiply_by_vector(g + 1, VECTOR_TOKENS)
                if ahead < N_GROUPS:
                    for first, when in ((0, 2 if g == 1 else 1), (PAIR, 4 if g == 1 else 3)):
                        if bank == when:
                            transpose_units(ahead, first, PAIR)
                            copy_units(nc.scalar.copy, ahead, first, PAIR)
                    if bank >= UNITS:
                        gate_unit(ahead, bank - UNITS)
                if bank == 5 and g + 1 < N_GROUPS:
                    quantise_units(g + 1, 0, UNITS)
                if bank == 7 and ahead < N_GROUPS:
                    multiply_by_gpsimd(ahead, VECTOR_TOKENS)
